import numpy as np
import ml_dtypes


def mxq(x, axis, fmt="e4m3"):
    dtype, down = {"e4m3": (ml_dtypes.float8_e4m3fn, 7), "e5m2": (ml_dtypes.float8_e5m2, 14)}[fmt]
    v = np.moveaxis(np.asarray(x, np.float32).astype(ml_dtypes.bfloat16).astype(np.float64), axis, -1)
    blocks = v.reshape(v.shape[:-1] + (-1, 32))
    amax = np.abs(blocks).max(-1, keepdims=True)
    byte = np.maximum(np.where(amax > 0, np.frexp(amax)[1] - 1 + 127, 0) - down, 1)
    scale = np.exp2(byte - 127.0)
    codes = (blocks / scale).astype(np.float32).astype(dtype).astype(np.float64)
    return np.moveaxis((codes * scale).reshape(v.shape), -1, axis)


WIDE = False


def mx_kscale(k):
    if not WIDE:
        return np.ones(k)
    levels = np.array([10, -10, 5, -5, 0])
    if k % 512:
        return np.exp2(np.random.permutation(np.resize(levels, k // 32))).repeat(32)
    a = np.empty((k // 512, 16))
    for p in range(k // 512):
        a[p, :8] = np.random.permutation(np.resize(levels, 8))
        for g in range(8):
            far = levels[np.abs(levels - a[p, g]) >= 10]
            a[p, g + 8] = far[np.random.randint(len(far))]
    return np.exp2(a.ravel()).repeat(32)


BF16 = ml_dtypes.bfloat16


def bf(x):
    return np.asarray(x, np.float32).astype(BF16)


def f64(x):
    return np.asarray(x).astype(np.float64)


B, HW, C, HID, WS, SS, HEADS = 8, 32, 512, 2048, 8, 4, 16
L = HW * HW
NH = HW // WS
EPS = 1e-5


def adain(x, scale, shift):
    m = x.mean(2, keepdims=True)
    s = np.std(x, axis=2, keepdims=True, ddof=1) + EPS
    return (x - m) / s * scale + shift


def setup_inputs():
    s = mx_kscale(C)
    return {"o_attn": bf(0.4 * np.random.standard_normal((NH * NH * B, WS * WS, C)) * s),
            "out_w": bf(np.random.standard_normal((C, C)) / np.sqrt(C) / s[None, :]),
            "out_b": bf(0.1 * np.random.standard_normal(C)),
            "ada1_scale": bf(1.0 + 0.1 * np.random.standard_normal((1, L, 1))),
            "ada1_shift": bf(0.1 * np.random.standard_normal((1, L, 1))),
            "x": bf(np.random.standard_normal((B, L, C)))}


def reference(o_attn, out_w, out_b, ada1_scale, ada1_shift, x):
    a = (mxq(f64(o_attn), 2, "e4m3") @ mxq(f64(out_w), 1, "e4m3").T) + f64(out_b)
    a = np.swapaxes(a.reshape(B, NH, NH, WS, WS, C), 2, 3).reshape(B, HW, HW, C)
    a = np.roll(a, (SS, SS), axis=(1, 2)).reshape(B, L, C)
    return f64(x) + adain(a, f64(ada1_scale), f64(ada1_shift))

@@ -1,0 +1,323 @@
+from contextlib import ExitStack
+
+import concourse.mybir as mybir
+from concourse.masks import make_identity
+
+F32 = mybir.dt.float32
+BF16 = mybir.dt.bfloat16
+U32 = mybir.dt.uint32
+U8 = mybir.dt.uint8
+FP8X4 = mybir.dt.float8_e4m3fn_x4
+ALU = mybir.AluOpType
+ACT = mybir.ActivationFunctionType
+
+P = 128
+C = 512
+IMAGES = 8
+GRID = 32
+WS = 8
+NWIN = GRID // WS
+SHIFT = 4
+BLOCKS = 4
+PAIRS = BLOCKS // 2
+EPS = 1e-5
+SHARED_BLOCKS = BLOCKS - 1
+FIRST_ROUND = -2
+LAST_LAG = 2
+O_AHEAD = 5
+X_AHEAD = 2
+LOAD_BUFS = 6
+
+FLOPS = 2 * IMAGES * GRID * GRID * C * C
+
+
+def rolled(count, shift):
+    pieces = [(0, shift, count - shift)]
+    if shift:
+        pieces.append((count - shift, 0, shift))
+    return pieces
+
+
+def make_window_permutation(nc, perm, ident, carry):
+    dst = perm.rearrange("p (wi rh rl wj) -> p wi rh rl wj", wi=NWIN, rh=2, rl=SHIFT, wj=NWIN)
+    src = ident.rearrange("p (wi wj rh rl) -> p wi rh rl wj", wi=NWIN, wj=NWIN, rh=2, rl=SHIFT)
+    for rh in range(2):
+        for wi_src, wi_dst, wi_len in rolled(NWIN, rh):
+            for wj_src, wj_dst, wj_len in rolled(NWIN, carry):
+                nc.vector.tensor_copy(
+                    out=dst[:, wi_dst : wi_dst + wi_len, 1 - rh, :, wj_dst : wj_dst + wj_len],
+                    in_=src[:, wi_src : wi_src + wi_len, rh, :, wj_src : wj_src + wj_len],
+                )
+
+
+def turn_rows(nc, turn, rows, perm):
+    banks = []
+    for pair in range(BLOCKS // 2):
+        turned = turn.tile([P, 2, 2, P], F32)
+        for a in range(2):
+            words = rows[:, 2 * pair + a, :].bitcast(F32)
+            for u in range(2):
+                nc.tensor.transpose(turned[:, a, u, :], words[:, u : 2 * P : 2], perm)
+        banks.append(turned)
+    return banks
+
+
+def group_words(copy_out, grouped, banks, pair):
+    grouped_words = grouped[:].bitcast(F32).rearrange("p (a j u) -> p a j u", a=BLOCKS, u=2)
+    copy_out(
+        out=grouped_words[:, 2 * pair : 2 * pair + 2, :, :],
+        in_=banks[pair][:].rearrange("p a u j -> p a j u"),
+    )
+
+
+def quantise_pair(nc, grouped, codes, scales, pair):
+    cols = slice(2 * P * pair, 2 * P * (pair + 1))
+    nc.vector.quantize_mx(
+        out=codes[:, cols].bitcast(FP8X4),
+        scales=scales[:, cols],
+        in_=grouped[:, 2 * C * pair : 2 * C * (pair + 1)],
+    )
+
+
+def tile_swintransformerblock_pb_t_kernel(
+    tc, o_attn, out_w, out_b, ada1_scale, ada1_shift, x, out
+):
+    nc = tc.nc
+    halves = 2 * IMAGES
+
+    o_rows = o_attn.flatten_outer_dims().rearrange("(b p c) k -> b p c k", p=P, c=WS)
+    x_rows = x.rearrange("b (p s) n -> b p s n", s=WS)
+    out_rows = out.rearrange("b (p s) n -> b p s n", s=WS)
+
+    def first_out_slot(h):
+        return BLOCKS * (1 - h % 2)
+
+    def out_slots(h):
+        return slice(first_out_slot(h), first_out_slot(h) + BLOCKS)
+
+    with ExitStack() as stack:
+        consts = stack.enter_context(tc.tile_pool(name="consts", bufs=1))
+        loads = stack.enter_context(tc.tile_pool(name="loads", bufs=LOAD_BUFS))
+        stage = stack.enter_context(tc.tile_pool(name="stage", bufs=2))
+        work = stack.enter_context(tc.tile_pool(name="work", bufs=3))
+        stats = stack.enter_context(tc.tile_pool(name="stats", bufs=4))
+        turn = stack.enter_context(tc.psum_pool(name="turn", bufs=4))
+        accs = stack.enter_context(tc.psum_pool(name="accs", bufs=4))
+        stack.enter_context(tc.manual_schedule())
+
+        kept = {}
+
+        def load_o(h):
+            o_tile = loads.tile([P, BLOCKS, C], BF16)
+            first = BLOCKS * (h % 2)
+            nc.sync.dma_start(out=o_tile[:], in_=o_rows[h // 2, :, first : first + BLOCKS, :])
+            kept["o", h] = o_tile
+
+        def load_x(h):
+            x_tile = loads.tile([P, BLOCKS, C], BF16)
+            nc.sync.dma_start(out=x_tile[:], in_=x_rows[h // 2, :, out_slots(h), :])
+            kept["x", h] = x_tile
+
+        w_rows = consts.tile([P, BLOCKS, C], BF16)
+        nc.sync.dma_start(out=w_rows[:], in_=out_w.rearrange("(a p) k -> p a k", p=P))
+        bias_row = consts.tile([P, C], BF16)
+        nc.vector.memset(bias_row[:], 0.0)
+        nc.sync.dma_start(out=bias_row[0:1, :], in_=out_b.rearrange("(o n) -> o n", o=1))
+        for h in range(O_AHEAD + FIRST_ROUND):
+            load_o(h)
+        gain = consts.tile([P, WS], BF16)
+        nc.sync.dma_start(
+            out=gain[:], in_=ada1_scale.flatten_outer_dims().rearrange("(p s) q -> p (s q)", p=P)
+        )
+        offset = consts.tile([P, WS], BF16)
+        nc.sync.dma_start(
+            out=offset[:], in_=ada1_shift.flatten_outer_dims().rearrange("(p s) q -> p (s q)", p=P)
+        )
+
+        ones = consts.tile([P, P], BF16)
+        nc.vector.memset(ones[:], 1.0)
+        table_warmer = consts.tile([P, 1], F32)
+        nc.scalar.activation(out=table_warmer[:], in_=ones[:, 0:1], func=ACT.Sqrt)
+
+        ident = consts.tile([P, P], F32)
+        make_identity(nc, ident[:])
+        perms = []
+        for carry in range(2):
+            perm = consts.tile([P, P], F32, name="perm%d" % carry)
+            make_window_permutation(nc, perm[:], ident[:], carry)
+            perms.append(perm)
+
+        w_codes = consts.tile([P, C], U32, align_bytes=64)
+        w_scales = consts.tile([P, C], U8, align_bytes=64)
+        w_banks = turn_rows(nc, turn, w_rows, ident[:])
+        w_grouped = stage.tile([P, BLOCKS * C], BF16, align_bytes=64, tag="grouped")
+        for pair in range(PAIRS):
+            group_words(nc.vector.tensor_copy, w_grouped, w_banks, pair)
+        for pair in range(PAIRS):
+            quantise_pair(nc, w_grouped, w_codes, w_scales, pair)
+
+        bias_bank = accs.tile([P, C], F32, tag="acc")
+        nc.tensor.matmul(bias_bank[:], lhsT=ones[:], rhs=bias_row[:], start=True, stop=True)
+        bias = consts.tile([P, C], F32)
+        nc.vector.tensor_copy(out=bias[:], in_=bias_bank[:])
+
+        def turn_half(h):
+            kept["banks", h] = turn_rows(nc, turn, kept["o", h], perms[h % 2][:])
+
+        def group_bank(h, pair):
+            if pair == 0:
+                grouped = stage.tile([P, BLOCKS * C], BF16, align_bytes=64, tag="grouped")
+                kept["grouped", h] = grouped
+            group_words(nc.scalar.copy, kept["grouped", h], kept["banks", h], pair)
+
+        def quantise(h, pair):
+            if pair == 0:
+                o_codes = stage.tile([P, BLOCKS * P], U32, align_bytes=64)
+                o_scales = stage.tile([P, BLOCKS * P], U8, align_bytes=64)
+                kept["codes", h] = o_codes
+                kept["scales", h] = o_scales
+            quantise_pair(nc, kept["grouped", h], kept["codes", h], kept["scales", h], pair)
+
+        def project(h):
+            for a in range(BLOCKS):
+                cols = slice(a * P, (a + 1) * P)
+                acc = accs.tile([P, C], F32, tag="acc")
+                nc.tensor.matmul_mx(
+                    out=acc[:],
+                    lhsT=kept["codes", h][:, cols].bitcast(FP8X4),
+                    lhsT_scale=kept["scales", h][:, cols],
+                    rhs=w_codes[:].bitcast(FP8X4),
+                    rhs_scale=w_scales[:],
+                    start=True,
+                    stop=True,
+                )
+                kept["acc", h, a] = acc
+
+        def add_bias(h):
+            t_all = work.tile([P, BLOCKS, C], F32)
+            t_sum = stats.tile([P, BLOCKS], F32)
+            for a in range(BLOCKS):
+                nc.vector.scalar_tensor_tensor(
+                    out=t_all[:, a, :],
+                    in0=kept["acc", h, a][:],
+                    scalar=1.0,
+                    in1=bias[:],
+                    op0=ALU.mult,
+                    op1=ALU.add,
+                    accum_out=t_sum[:, a : a + 1],
+                )
+            kept["t", h] = t_all
+            kept["t_sum", h] = t_sum
+
+        def squared_deviations(h):
+            squares = stage.tile([P, BLOCKS, C], BF16)
+            dev_sq = stats.tile([P, BLOCKS], F32)
+            for a in range(BLOCKS):
+                nc.scalar.activation(
+                    out=squares[:, a, :],
+                    in_=kept["t", h][:, a, :],
+                    func=ACT.Square,
+                    bias=kept["t_sum", h][:, a : a + 1],
+                    scale=-1.0 * C,
+                    accum_out=dev_sq[:, a : a + 1],
+                )
+            kept["dev_sq", h] = dev_sq
+
+        def standard_deviation(h):
+            std = stats.tile([P, BLOCKS], F32)
+            nc.scalar.activation(
+                out=std[:], in_=kept["dev_sq", h][:], func=ACT.Sqrt, scale=1.0 / ((C - 1) * C * C)
+            )
+            kept["std", h] = std
+
+        def slope_step(h, step):
+            if step == 0:
+                slope = stats.tile([P, BLOCKS], F32)
+                level = stats.tile([P, BLOCKS], F32)
+                kept["slope", h] = slope
+                kept["level", h] = level
+                nc.vector.tensor_scalar_add(out=slope[:], in0=kept["std", h][:], scalar1=EPS)
+            slope = kept["slope", h]
+            level = kept["level", h]
+            if step == 1:
+                nc.vector.reciprocal(out=slope[:], in_=slope[:])
+            if step == 2:
+                nc.vector.tensor_mul(out=slope[:], in0=slope[:], in1=gain[:, out_slots(h)])
+            if step == 3:
+                nc.vector.tensor_mul(out=level[:], in0=kept["t_sum", h][:], in1=slope[:])
+            if step == 4:
+                nc.vector.scalar_tensor_tensor(
+                    out=level[:],
+                    in0=level[:],
+                    scalar=-1.0 / C,
+                    in1=offset[:, out_slots(h)],
+                    op0=ALU.mult,
+                    op1=ALU.add,
+                )
+
+        def normalise(h):
+            result = work.tile([P, BLOCKS, C], F32)
+            for a in range(SHARED_BLOCKS):
+                nc.scalar.activation(
+                    out=result[:, a, :],
+                    in_=kept["t", h][:, a, :],
+                    func=ACT.Identity,
+                    bias=kept["level", h][:, a : a + 1],
+                    scale=kept["slope", h][:, a : a + 1],
+                )
+            kept["result", h] = result
+
+        def finish_last_block(h):
+            last = BLOCKS - 1
+            result = kept["result", h]
+            nc.gpsimd.tensor_scalar(
+                out=result[:, last, :],
+                in0=kept["t", h][:, last, :],
+                scalar1=kept["slope", h][:, last : last + 1],
+                scalar2=kept["level", h][:, last : last + 1],
+                op0=ALU.mult,
+                op1=ALU.add,
+            )
+            nc.gpsimd.tensor_add(
+                out=result[:, last, :], in0=result[:, last, :], in1=kept["x", h][:, last, :]
+            )
+
+        def add_residual(h, a):
+            result = kept["result", h]
+            nc.vector.tensor_add(out=result[:, a, :], in0=result[:, a, :], in1=kept["x", h][:, a, :])
+
+        def store(h, pair):
+            first = first_out_slot(h) + 2 * pair
+            nc.sync.dma_start(
+                out=out_rows[h // 2, :, first : first + 2, :],
+                in_=kept["result", h][:, 2 * pair : 2 * pair + 2, :],
+            )
+
+        def run(stage_of_half, h, *more):
+            if 0 <= h < halves:
+                stage_of_half(h, *more)
+
+        for i in range(FIRST_ROUND, halves + LAST_LAG):
+            run(load_o, i + O_AHEAD)
+            run(load_x, i + X_AHEAD)
+            run(turn_half, i + 2)
+            run(squared_deviations, i - 1)
+            run(group_bank, i + 1, 0)
+            run(standard_deviation, i - 1)
+            run(group_bank, i + 1, 1)
+            run(normalise, i - 2)
+            run(finish_last_block, i - 2)
+            run(add_bias, i)
+            run(slope_step, i - 1, 0)
+            run(quantise, i + 1, 0)
+            run(slope_step, i - 1, 1)
+            run(quantise, i + 1, 1)
+            run(project, i + 1)
+            run(slope_step, i - 1, 2)
+            run(add_residual, i - 2, 0)
+            run(slope_step, i - 1, 3)
+            run(add_residual, i - 2, 1)
+            run(store, i - 2, 0)
+            run(slope_step, i - 1, 4)
+            run(add_residual, i - 2, 2)
+            run(store, i - 2, 1)

@@ -21,11 +21,12 @@ SHIFT = 4
 BLOCKS = 4
 PAIRS = BLOCKS // 2
 EPS = 1e-5
-SHARED_BLOCKS = BLOCKS - 1
+SCALAR_BLOCKS = (0, 1)
+GPSIMD_BLOCKS = slice(2, BLOCKS)
 FIRST_ROUND = -2
 LAST_LAG = 2
 O_AHEAD = 5
-X_AHEAD = 2
+X_AHEAD = 1
 LOAD_BUFS = 6
 
 FLOPS = 2 * IMAGES * GRID * GRID * C * C
@@ -50,23 +51,20 @@ def make_window_permutation(nc, perm, ident, carry):
                 )
 
 
-def turn_rows(nc, turn, rows, perm):
-    banks = []
-    for pair in range(BLOCKS // 2):
-        turned = turn.tile([P, 2, 2, P], F32)
-        for a in range(2):
-            words = rows[:, 2 * pair + a, :].bitcast(F32)
-            for u in range(2):
-                nc.tensor.transpose(turned[:, a, u, :], words[:, u : 2 * P : 2], perm)
-        banks.append(turned)
-    return banks
+def turn_pair(nc, turn, rows, perm, pair):
+    turned = turn.tile([P, 2, 2, P], F32)
+    for a in range(2):
+        words = rows[:, 2 * pair + a, :].bitcast(F32)
+        for u in range(2):
+            nc.tensor.transpose(turned[:, a, u, :], words[:, u : 2 * P : 2], perm)
+    return turned
 
 
-def group_words(copy_out, grouped, banks, pair):
+def group_words(copy_out, grouped, bank, pair):
     grouped_words = grouped[:].bitcast(F32).rearrange("p (a j u) -> p a j u", a=BLOCKS, u=2)
     copy_out(
         out=grouped_words[:, 2 * pair : 2 * pair + 2, :, :],
-        in_=banks[pair][:].rearrange("p a u j -> p a j u"),
+        in_=bank[:].rearrange("p a u j -> p a j u"),
     )
 
 
@@ -99,10 +97,11 @@ def tile_swintransformerblock_pb_t_kernel(
         consts = stack.enter_context(tc.tile_pool(name="consts", bufs=1))
         loads = stack.enter_context(tc.tile_pool(name="loads", bufs=LOAD_BUFS))
         stage = stack.enter_context(tc.tile_pool(name="stage", bufs=2))
-        work = stack.enter_context(tc.tile_pool(name="work", bufs=3))
+        work = stack.enter_context(tc.tile_pool(name="work", bufs=4))
         stats = stack.enter_context(tc.tile_pool(name="stats", bufs=4))
-        turn = stack.enter_context(tc.psum_pool(name="turn", bufs=4))
+        turn = stack.enter_context(tc.psum_pool(name="turn", bufs=2))
         accs = stack.enter_context(tc.psum_pool(name="accs", bufs=4))
+        copies = stack.enter_context(tc.psum_pool(name="copies", bufs=2))
         stack.enter_context(tc.manual_schedule())
 
         kept = {}
@@ -110,7 +109,12 @@ def tile_swintransformerblock_pb_t_kernel(
         def load_o(h):
             o_tile = loads.tile([P, BLOCKS, C], BF16)
             first = BLOCKS * (h % 2)
-            nc.sync.dma_start(out=o_tile[:], in_=o_rows[h // 2, :, first : first + BLOCKS, :])
+            step = 2 if h == 0 else BLOCKS
+            for a in range(0, BLOCKS, step):
+                nc.sync.dma_start(
+                    out=o_tile[:, a : a + step, :],
+                    in_=o_rows[h // 2, :, first + a : first + a + step, :],
+                )
             kept["o", h] = o_tile
 
         def load_x(h):
@@ -118,11 +122,13 @@ def tile_swintransformerblock_pb_t_kernel(
             nc.sync.dma_start(out=x_tile[:], in_=x_rows[h // 2, :, out_slots(h), :])
             kept["x", h] = x_tile
 
-        w_rows = consts.tile([P, BLOCKS, C], BF16)
-        nc.sync.dma_start(out=w_rows[:], in_=out_w.rearrange("(a p) k -> p a k", p=P))
         bias_row = consts.tile([P, C], BF16)
         nc.vector.memset(bias_row[:], 0.0)
         nc.sync.dma_start(out=bias_row[0:1, :], in_=out_b.rearrange("(o n) -> o n", o=1))
+        w_rows = consts.tile([P, BLOCKS, C], BF16)
+        w_view = out_w.rearrange("(a p) k -> p a k", p=P)
+        for a in range(0, BLOCKS, 2):
+            nc.sync.dma_start(out=w_rows[:, a : a + 2, :], in_=w_view[:, a : a + 2, :])
         for h in range(O_AHEAD + FIRST_ROUND):
             load_o(h)
         gain = consts.tile([P, WS], BF16)
@@ -141,34 +147,36 @@ def tile_swintransformerblock_pb_t_kernel(
 
         ident = consts.tile([P, P], F32)
         make_identity(nc, ident[:])
+        ident_bf16 = consts.tile([P, P], BF16)
         perms = []
         for carry in range(2):
             perm = consts.tile([P, P], F32, name="perm%d" % carry)
             make_window_permutation(nc, perm[:], ident[:], carry)
             perms.append(perm)
-
-        w_codes = consts.tile([P, C], U32, align_bytes=64)
-        w_scales = consts.tile([P, C], U8, align_bytes=64)
-        w_banks = turn_rows(nc, turn, w_rows, ident[:])
-        w_grouped = stage.tile([P, BLOCKS * C], BF16, align_bytes=64, tag="grouped")
-        for pair in range(PAIRS):
-            group_words(nc.vector.tensor_copy, w_grouped, w_banks, pair)
-        for pair in range(PAIRS):
-            quantise_pair(nc, w_grouped, w_codes, w_scales, pair)
+        nc.vector.tensor_copy(out=ident_bf16[:], in_=ident[:])
 
         bias_bank = accs.tile([P, C], F32, tag="acc")
         nc.tensor.matmul(bias_bank[:], lhsT=ones[:], rhs=bias_row[:], start=True, stop=True)
         bias = consts.tile([P, C], F32)
         nc.vector.tensor_copy(out=bias[:], in_=bias_bank[:])
 
-        def turn_half(h):
-            kept["banks", h] = turn_rows(nc, turn, kept["o", h], perms[h % 2][:])
+        w_codes = consts.tile([P, C], U32, align_bytes=64)
+        w_scales = consts.tile([P, C], U8, align_bytes=64)
+        w_grouped = stage.tile([P, BLOCKS * C], BF16, align_bytes=64, tag="grouped")
+        for pair, copy_out in enumerate((nc.vector.tensor_copy, nc.scalar.copy)):
+            w_bank = turn_pair(nc, turn, w_rows, ident[:], pair)
+            group_words(copy_out, w_grouped, w_bank, pair)
+        for pair in range(PAIRS):
+            quantise_pair(nc, w_grouped, w_codes, w_scales, pair)
+
+        def turn_bank(h, pair):
+            kept["bank", h, pair] = turn_pair(nc, turn, kept["o", h], perms[h % 2][:], pair)
 
         def group_bank(h, pair):
             if pair == 0:
                 grouped = stage.tile([P, BLOCKS * C], BF16, align_bytes=64, tag="grouped")
                 kept["grouped", h] = grouped
-            group_words(nc.scalar.copy, kept["grouped", h], kept["banks", h], pair)
+            group_words(nc.scalar.copy, kept["grouped", h], kept["bank", h, pair], pair)
 
         def quantise(h, pair):
             if pair == 0:
@@ -230,61 +238,98 @@ def tile_swintransformerblock_pb_t_kernel(
             )
             kept["std", h] = std
 
+        def add_eps(h):
+            std = kept["std", h]
+            nc.scalar.add(std[:], std[:], EPS)
+
         def slope_step(h, step):
             if step == 0:
                 slope = stats.tile([P, BLOCKS], F32)
                 level = stats.tile([P, BLOCKS], F32)
                 kept["slope", h] = slope
                 kept["level", h] = level
-                nc.vector.tensor_scalar_add(out=slope[:], in0=kept["std", h][:], scalar1=EPS)
+                nc.vector.reciprocal(out=slope[:], in_=kept["std", h][:])
             slope = kept["slope", h]
             level = kept["level", h]
             if step == 1:
-                nc.vector.reciprocal(out=slope[:], in_=slope[:])
-            if step == 2:
                 nc.vector.tensor_mul(out=slope[:], in0=slope[:], in1=gain[:, out_slots(h)])
-            if step == 3:
-                nc.vector.tensor_mul(out=level[:], in0=kept["t_sum", h][:], in1=slope[:])
-            if step == 4:
+            if step == 2:
                 nc.vector.scalar_tensor_tensor(
                     out=level[:],
-                    in0=level[:],
+                    in0=kept["t_sum", h][:],
                     scalar=-1.0 / C,
-                    in1=offset[:, out_slots(h)],
+                    in1=slope[:],
                     op0=ALU.mult,
-                    op1=ALU.add,
+                    op1=ALU.mult,
                 )
 
-        def normalise(h):
-            result = work.tile([P, BLOCKS, C], F32)
-            for a in range(SHARED_BLOCKS):
-                nc.scalar.activation(
-                    out=result[:, a, :],
-                    in_=kept["t", h][:, a, :],
-                    func=ACT.Identity,
-                    bias=kept["level", h][:, a : a + 1],
-                    scale=kept["slope", h][:, a : a + 1],
-                )
-            kept["result", h] = result
+        def scalar_normalise(h, a):
+            if a == SCALAR_BLOCKS[0]:
+                result = work.tile([P, BLOCKS, C], F32)
+                kept["result", h] = result
+            nc.scalar.activation(
+                out=kept["result", h][:, a, :],
+                in_=kept["t", h][:, a, :],
+                func=ACT.Identity,
+                bias=kept["level", h][:, a : a + 1],
+                scale=kept["slope", h][:, a : a + 1],
+            )
 
-        def finish_last_block(h):
-            last = BLOCKS - 1
-            result = kept["result", h]
-            nc.gpsimd.tensor_scalar(
-                out=result[:, last, :],
-                in0=kept["t", h][:, last, :],
-                scalar1=kept["slope", h][:, last : last + 1],
-                scalar2=kept["level", h][:, last : last + 1],
+        def normalise_on(engine, h, a, level):
+            engine.tensor_scalar(
+                out=kept["result", h][:, a, :],
+                in0=kept["t", h][:, a, :],
+                scalar1=kept["slope", h][:, a : a + 1],
+                scalar2=level,
                 op0=ALU.mult,
                 op1=ALU.add,
             )
+
+        def gpsimd_blocks(h):
+            shifted = stats.tile([P, 2], F32)
+            first = first_out_slot(h)
             nc.gpsimd.tensor_add(
-                out=result[:, last, :], in0=result[:, last, :], in1=kept["x", h][:, last, :]
+                out=shifted[:],
+                in0=kept["level", h][:, GPSIMD_BLOCKS],
+                in1=offset[:, first + GPSIMD_BLOCKS.start : first + GPSIMD_BLOCKS.stop],
             )
+            result = kept["result", h]
+            for j in range(2):
+                normalise_on(nc.gpsimd, h, GPSIMD_BLOCKS.start + j, shifted[:, j : j + 1])
+            for a in range(GPSIMD_BLOCKS.start, GPSIMD_BLOCKS.stop):
+                nc.gpsimd.tensor_add(
+                    out=result[:, a, :], in0=result[:, a, :], in1=kept["x", h][:, a, :]
+                )
+
+        def through_psum(h, a):
+            return a in SCALAR_BLOCKS and (a == 1 or h % 2 == 1)
+
+        def copy_x(h):
+            for a in SCALAR_BLOCKS:
+                if through_psum(h, a):
+                    x_bank = copies.tile([P, C], F32)
+                    nc.tensor.matmul(
+                        x_bank[:], lhsT=ident_bf16[:], rhs=kept["x", h][:, a, :], start=True, stop=True
+                    )
+                    kept["x_bank", h, a] = x_bank
 
         def add_residual(h, a):
             result = kept["result", h]
-            nc.vector.tensor_add(out=result[:, a, :], in0=result[:, a, :], in1=kept["x", h][:, a, :])
+            slot = first_out_slot(h) + a
+            x_block = kept["x_bank", h, a][:] if through_psum(h, a) else kept["x", h][:, a, :]
+            nc.vector.scalar_tensor_tensor(
+                out=result[:, a, :],
+                in0=result[:, a, :],
+                scalar=offset[:, slot : slot + 1],
+                in1=x_block,
+                op0=ALU.add,
+                op1=ALU.add,
+            )
+
+        def add_residuals(h, by_psum):
+            for a in SCALAR_BLOCKS:
+                if through_psum(h, a) == by_psum:
+                    add_residual(h, a)
 
         def store(h, pair):
             first = first_out_slot(h) + 2 * pair
@@ -293,6 +338,14 @@ def tile_swintransformerblock_pb_t_kernel(
                 in_=kept["result", h][:, 2 * pair : 2 * pair + 2, :],
             )
 
+        def finish_final_half(h):
+            for a in range(GPSIMD_BLOCKS.start, GPSIMD_BLOCKS.stop):
+                normalise_on(nc.vector, h, a, kept["level", h][:, a : a + 1])
+            for pair in reversed(range(PAIRS)):
+                for a in range(2 * pair, 2 * pair + 2):
+                    add_residual(h, a)
+                store(h, pair)
+
         def run(stage_of_half, h, *more):
             if 0 <= h < halves:
                 stage_of_half(h, *more)
@@ -300,24 +353,29 @@ def tile_swintransformerblock_pb_t_kernel(
         for i in range(FIRST_ROUND, halves + LAST_LAG):
             run(load_o, i + O_AHEAD)
             run(load_x, i + X_AHEAD)
-            run(turn_half, i + 2)
             run(squared_deviations, i - 1)
-            run(group_bank, i + 1, 0)
             run(standard_deviation, i - 1)
+            run(group_bank, i + 1, 0)
+            run(turn_bank, i + 2, 0)
+            run(add_eps, i - 1)
             run(group_bank, i + 1, 1)
-            run(normalise, i - 2)
-            run(finish_last_block, i - 2)
+            run(turn_bank, i + 2, 1)
+            for a in SCALAR_BLOCKS:
+                run(scalar_normalise, i - 2, a)
+            run(copy_x, i - 2)
+            if i - 2 < halves - 1:
+                run(gpsimd_blocks, i - 2)
             run(add_bias, i)
+            if i - 2 < halves - 1:
+                run(add_residuals, i - 2, True)
             run(slope_step, i - 1, 0)
             run(quantise, i + 1, 0)
             run(slope_step, i - 1, 1)
             run(quantise, i + 1, 1)
             run(project, i + 1)
             run(slope_step, i - 1, 2)
-            run(add_residual, i - 2, 0)
-            run(slope_step, i - 1, 3)
-            run(add_residual, i - 2, 1)
-            run(store, i - 2, 0)
-            run(slope_step, i - 1, 4)
-            run(add_residual, i - 2, 2)
-            run(store, i - 2, 1)
+            if i - 2 < halves - 1:
+                run(add_residuals, i - 2, False)
+                for pair in range(PAIRS):
+                    run(store, i - 2, pair)
+        finish_final_half(halves - 1)

@@ -21,12 +21,11 @@ SHIFT = 4
 BLOCKS = 4
 PAIRS = BLOCKS // 2
 EPS = 1e-5
-SCALAR_BLOCKS = (0, 1)
-GPSIMD_BLOCKS = slice(2, BLOCKS)
-FIRST_ROUND = -2
-LAST_LAG = 2
-O_AHEAD = 5
-X_AHEAD = 1
+SCALAR_BLOCKS = (0, 2, 3)
+VECTOR_BLOCK = 1
+GPSIMD_BLOCKS = slice(1, BLOCKS)
+FULL_ROUNDS = 2 * IMAGES - 2
+O_AHEAD = 3
 LOAD_BUFS = 6
 
 FLOPS = 2 * IMAGES * GRID * GRID * C * C
@@ -97,8 +96,8 @@ def tile_swintransformerblock_pb_t_kernel(
         consts = stack.enter_context(tc.tile_pool(name="consts", bufs=1))
         loads = stack.enter_context(tc.tile_pool(name="loads", bufs=LOAD_BUFS))
         stage = stack.enter_context(tc.tile_pool(name="stage", bufs=2))
-        work = stack.enter_context(tc.tile_pool(name="work", bufs=4))
-        stats = stack.enter_context(tc.tile_pool(name="stats", bufs=4))
+        work = stack.enter_context(tc.tile_pool(name="work", bufs=5))
+        stats = stack.enter_context(tc.tile_pool(name="stats", bufs=5))
         turn = stack.enter_context(tc.psum_pool(name="turn", bufs=2))
         accs = stack.enter_context(tc.psum_pool(name="accs", bufs=4))
         copies = stack.enter_context(tc.psum_pool(name="copies", bufs=2))
@@ -129,7 +128,7 @@ def tile_swintransformerblock_pb_t_kernel(
         w_view = out_w.rearrange("(a p) k -> p a k", p=P)
         for a in range(0, BLOCKS, 2):
             nc.sync.dma_start(out=w_rows[:, a : a + 2, :], in_=w_view[:, a : a + 2, :])
-        for h in range(O_AHEAD + FIRST_ROUND):
+        for h in range(O_AHEAD):
             load_o(h)
         gain = consts.tile([P, WS], BF16)
         nc.sync.dma_start(
@@ -172,11 +171,11 @@ def tile_swintransformerblock_pb_t_kernel(
         def turn_bank(h, pair):
             kept["bank", h, pair] = turn_pair(nc, turn, kept["o", h], perms[h % 2][:], pair)
 
-        def group_bank(h, pair):
+        def group_bank(h, pair, copy_out):
             if pair == 0:
                 grouped = stage.tile([P, BLOCKS * C], BF16, align_bytes=64, tag="grouped")
                 kept["grouped", h] = grouped
-            group_words(nc.scalar.copy, kept["grouped", h], kept["bank", h, pair], pair)
+            group_words(copy_out, kept["grouped", h], kept["bank", h, pair], pair)
 
         def quantise(h, pair):
             if pair == 0:
@@ -186,8 +185,8 @@ def tile_swintransformerblock_pb_t_kernel(
                 kept["scales", h] = o_scales
             quantise_pair(nc, kept["grouped", h], kept["codes", h], kept["scales", h], pair)
 
-        def project(h):
-            for a in range(BLOCKS):
+        def project(h, pair):
+            for a in range(2 * pair, 2 * pair + 2):
                 cols = slice(a * P, (a + 1) * P)
                 acc = accs.tile([P, C], F32, tag="acc")
                 nc.tensor.matmul_mx(
@@ -217,19 +216,20 @@ def tile_swintransformerblock_pb_t_kernel(
             kept["t", h] = t_all
             kept["t_sum", h] = t_sum
 
-        def squared_deviations(h):
-            squares = stage.tile([P, BLOCKS, C], BF16)
-            dev_sq = stats.tile([P, BLOCKS], F32)
-            for a in range(BLOCKS):
+        def squared_deviations(h, blocks):
+            if ("dev_sq", h) not in kept:
+                dev_sq = stats.tile([P, BLOCKS], F32)
+                kept["dev_sq", h] = dev_sq
+            for a in blocks:
+                squares = stage.tile([P, C], BF16)
                 nc.scalar.activation(
-                    out=squares[:, a, :],
+                    out=squares[:],
                     in_=kept["t", h][:, a, :],
                     func=ACT.Square,
                     bias=kept["t_sum", h][:, a : a + 1],
                     scale=-1.0 * C,
-                    accum_out=dev_sq[:, a : a + 1],
+                    accum_out=kept["dev_sq", h][:, a : a + 1],
                 )
-            kept["dev_sq", h] = dev_sq
 
         def standard_deviation(h):
             std = stats.tile([P, BLOCKS], F32)
@@ -262,120 +262,164 @@ def tile_swintransformerblock_pb_t_kernel(
                     op0=ALU.mult,
                     op1=ALU.mult,
                 )
+            if step == 3:
+                nc.vector.tensor_add(out=level[:], in0=level[:], in1=offset[:, out_slots(h)])
 
-        def scalar_normalise(h, a):
-            if a == SCALAR_BLOCKS[0]:
+        def result_of(h):
+            if ("result", h) not in kept:
                 result = work.tile([P, BLOCKS, C], F32)
                 kept["result", h] = result
-            nc.scalar.activation(
-                out=kept["result", h][:, a, :],
-                in_=kept["t", h][:, a, :],
-                func=ACT.Identity,
-                bias=kept["level", h][:, a : a + 1],
-                scale=kept["slope", h][:, a : a + 1],
-            )
+            return kept["result", h]
 
-        def normalise_on(engine, h, a, level):
-            engine.tensor_scalar(
-                out=kept["result", h][:, a, :],
+        def scalar_normalise(h, blocks):
+            for a in blocks:
+                nc.scalar.activation(
+                    out=result_of(h)[:, a, :],
+                    in_=kept["t", h][:, a, :],
+                    func=ACT.Identity,
+                    bias=kept["level", h][:, a : a + 1],
+                    scale=kept["slope", h][:, a : a + 1],
+                )
+
+        def vector_normalise(h, a):
+            nc.vector.tensor_scalar(
+                out=result_of(h)[:, a, :],
                 in0=kept["t", h][:, a, :],
                 scalar1=kept["slope", h][:, a : a + 1],
-                scalar2=level,
+                scalar2=kept["level", h][:, a : a + 1],
                 op0=ALU.mult,
                 op1=ALU.add,
             )
 
-        def gpsimd_blocks(h):
-            shifted = stats.tile([P, 2], F32)
-            first = first_out_slot(h)
+        def gpsimd_add_x(h, blocks):
+            result = kept["result", h]
             nc.gpsimd.tensor_add(
-                out=shifted[:],
-                in0=kept["level", h][:, GPSIMD_BLOCKS],
-                in1=offset[:, first + GPSIMD_BLOCKS.start : first + GPSIMD_BLOCKS.stop],
+                out=result[:, blocks, :], in0=result[:, blocks, :], in1=kept["x", h][:, blocks, :]
             )
+
+        def vector_add_x(h, blocks):
             result = kept["result", h]
-            for j in range(2):
-                normalise_on(nc.gpsimd, h, GPSIMD_BLOCKS.start + j, shifted[:, j : j + 1])
-            for a in range(GPSIMD_BLOCKS.start, GPSIMD_BLOCKS.stop):
-                nc.gpsimd.tensor_add(
-                    out=result[:, a, :], in0=result[:, a, :], in1=kept["x", h][:, a, :]
+            for a in blocks:
+                x_bank = copies.tile([P, C], F32)
+                nc.tensor.matmul(
+                    x_bank[:], lhsT=ident_bf16[:], rhs=kept["x", h][:, a, :], start=True, stop=True
                 )
+                nc.vector.tensor_add(out=result[:, a, :], in0=result[:, a, :], in1=x_bank[:])
 
-        def through_psum(h, a):
-            return a in SCALAR_BLOCKS and (a == 1 or h % 2 == 1)
-
-        def copy_x(h):
-            for a in SCALAR_BLOCKS:
-                if through_psum(h, a):
-                    x_bank = copies.tile([P, C], F32)
-                    nc.tensor.matmul(
-                        x_bank[:], lhsT=ident_bf16[:], rhs=kept["x", h][:, a, :], start=True, stop=True
-                    )
-                    kept["x_bank", h, a] = x_bank
-
-        def add_residual(h, a):
-            result = kept["result", h]
-            slot = first_out_slot(h) + a
-            x_block = kept["x_bank", h, a][:] if through_psum(h, a) else kept["x", h][:, a, :]
-            nc.vector.scalar_tensor_tensor(
-                out=result[:, a, :],
-                in0=result[:, a, :],
-                scalar=offset[:, slot : slot + 1],
-                in1=x_block,
-                op0=ALU.add,
-                op1=ALU.add,
-            )
-
-        def add_residuals(h, by_psum):
-            for a in SCALAR_BLOCKS:
-                if through_psum(h, a) == by_psum:
-                    add_residual(h, a)
-
-        def store(h, pair):
-            first = first_out_slot(h) + 2 * pair
+        def store(h, first, count):
+            slot = first_out_slot(h) + first
             nc.sync.dma_start(
-                out=out_rows[h // 2, :, first : first + 2, :],
-                in_=kept["result", h][:, 2 * pair : 2 * pair + 2, :],
+                out=out_rows[h // 2, :, slot : slot + count, :],
+                in_=kept["result", h][:, first : first + count, :],
             )
-
-        def finish_final_half(h):
-            for a in range(GPSIMD_BLOCKS.start, GPSIMD_BLOCKS.stop):
-                normalise_on(nc.vector, h, a, kept["level", h][:, a : a + 1])
-            for pair in reversed(range(PAIRS)):
-                for a in range(2 * pair, 2 * pair + 2):
-                    add_residual(h, a)
-                store(h, pair)
 
         def run(stage_of_half, h, *more):
             if 0 <= h < halves:
                 stage_of_half(h, *more)
 
-        for i in range(FIRST_ROUND, halves + LAST_LAG):
+        turn_bank(0, 0)
+        group_bank(0, 0, nc.scalar.copy)
+        turn_bank(0, 1)
+        group_bank(0, 1, nc.scalar.copy)
+        quantise(0, 0)
+        turn_bank(1, 0)
+        project(0, 0)
+        quantise(0, 1)
+        group_bank(1, 0, nc.scalar.copy)
+        turn_bank(1, 1)
+        project(0, 1)
+        group_bank(1, 1, nc.scalar.copy)
+
+        for i in range(FULL_ROUNDS):
             run(load_o, i + O_AHEAD)
-            run(load_x, i + X_AHEAD)
-            run(squared_deviations, i - 1)
-            run(standard_deviation, i - 1)
-            run(group_bank, i + 1, 0)
+            load_x(i)
+            run(squared_deviations, i - 1, range(BLOCKS))
             run(turn_bank, i + 2, 0)
+            run(group_bank, i + 2, 0, nc.scalar.copy)
+            run(standard_deviation, i - 1)
+            run(scalar_normalise, i - 2, SCALAR_BLOCKS[:1])
             run(add_eps, i - 1)
-            run(group_bank, i + 1, 1)
-            run(turn_bank, i + 2, 1)
-            for a in SCALAR_BLOCKS:
-                run(scalar_normalise, i - 2, a)
-            run(copy_x, i - 2)
-            if i - 2 < halves - 1:
-                run(gpsimd_blocks, i - 2)
-            run(add_bias, i)
-            if i - 2 < halves - 1:
-                run(add_residuals, i - 2, True)
+            run(scalar_normalise, i - 2, SCALAR_BLOCKS[1:])
+            if i < 2:
+                run(turn_bank, i + 2, 1)
+                run(group_bank, i + 2, 1, nc.scalar.copy)
+            run(gpsimd_add_x, i - 3, GPSIMD_BLOCKS)
+            for pair in range(PAIRS):
+                run(store, i - 3, 2 * pair, 2)
+            add_bias(i)
+            if i >= 2:
+                run(turn_bank, i + 2, 1)
+                run(group_bank, i + 2, 1, nc.vector.tensor_copy)
+            run(vector_add_x, i - 2, (0,))
             run(slope_step, i - 1, 0)
-            run(quantise, i + 1, 0)
+            quantise(i + 1, 0)
             run(slope_step, i - 1, 1)
-            run(quantise, i + 1, 1)
-            run(project, i + 1)
+            quantise(i + 1, 1)
+            for pair in range(PAIRS):
+                project(i + 1, pair)
             run(slope_step, i - 1, 2)
-            if i - 2 < halves - 1:
-                run(add_residuals, i - 2, False)
-                for pair in range(PAIRS):
-                    run(store, i - 2, pair)
-        finish_final_half(halves - 1)
+            run(slope_step, i - 1, 3)
+            run(vector_normalise, i - 2, VECTOR_BLOCK)
+
+        e = halves - 1
+        for h in (e - 1, e):
+            load_x(h)
+        squared_deviations(e - 2, range(BLOCKS))
+        standard_deviation(e - 2)
+        add_eps(e - 2)
+        scalar_normalise(e - 3, SCALAR_BLOCKS)
+        gpsimd_add_x(e - 4, GPSIMD_BLOCKS)
+        store(e - 4, 0, 2)
+        store(e - 4, 2, 2)
+        add_bias(e - 1)
+        vector_add_x(e - 3, (0,))
+        slope_step(e - 2, 0)
+        quantise(e, 0)
+        slope_step(e - 2, 1)
+        quantise(e, 1)
+        for pair in range(PAIRS):
+            project(e, pair)
+        slope_step(e - 2, 2)
+        slope_step(e - 2, 3)
+        vector_normalise(e - 3, VECTOR_BLOCK)
+
+        squared_deviations(e - 1, range(BLOCKS))
+        standard_deviation(e - 1)
+        add_eps(e - 1)
+        gpsimd_add_x(e - 3, GPSIMD_BLOCKS)
+        store(e - 3, 0, 2)
+        store(e - 3, 2, 2)
+        add_bias(e)
+        scalar_normalise(e - 2, (0, 1))
+        squared_deviations(e, (0, 1))
+        scalar_normalise(e - 2, (2,))
+        squared_deviations(e, (2, 3))
+        standard_deviation(e)
+        add_eps(e)
+        vector_add_x(e - 2, (0, 1))
+        store(e - 2, 0, 2)
+        slope_step(e - 1, 0)
+        vector_normalise(e - 2, 3)
+        slope_step(e - 1, 1)
+        vector_add_x(e - 2, (2,))
+        slope_step(e - 1, 2)
+        vector_add_x(e - 2, (3,))
+        store(e - 2, 2, 2)
+        slope_step(e - 1, 3)
+        slope_step(e, 0)
+        vector_normalise(e - 1, 2)
+        slope_step(e, 1)
+        vector_normalise(e - 1, 3)
+        slope_step(e, 2)
+        slope_step(e, 3)
+        scalar_normalise(e - 1, (0, 1))
+        gpsimd_add_x(e - 1, slice(0, 2))
+        store(e - 1, 0, 2)
+        vector_add_x(e - 1, (2, 3))
+        store(e - 1, 2, 2)
+        scalar_normalise(e, range(BLOCKS))
+        vector_add_x(e, (0, 1))
+        store(e, 0, 2)
+        for a in (2, 3):
+            vector_add_x(e, (a,))
+            store(e, a, 1)

@@ -21,12 +21,12 @@ SHIFT = 4
 BLOCKS = 4
 PAIRS = BLOCKS // 2
 EPS = 1e-5
-SCALAR_BLOCKS = (0, 2, 3)
-VECTOR_BLOCK = 1
-GPSIMD_BLOCKS = slice(1, BLOCKS)
-FULL_ROUNDS = 2 * IMAGES - 2
+SCALAR_BLOCKS = (0, 1)
+GPSIMD_BLOCKS = (2, 3)
+LAST = BLOCKS - 1
+FULL_ROUNDS = 2 * IMAGES - 1
 O_AHEAD = 3
-LOAD_BUFS = 6
+LOAD_BUFS = 7
 
 FLOPS = 2 * IMAGES * GRID * GRID * C * C
 
@@ -96,8 +96,9 @@ def tile_swintransformerblock_pb_t_kernel(
         consts = stack.enter_context(tc.tile_pool(name="consts", bufs=1))
         loads = stack.enter_context(tc.tile_pool(name="loads", bufs=LOAD_BUFS))
         stage = stack.enter_context(tc.tile_pool(name="stage", bufs=2))
-        work = stack.enter_context(tc.tile_pool(name="work", bufs=5))
-        stats = stack.enter_context(tc.tile_pool(name="stats", bufs=5))
+        sums = stack.enter_context(tc.tile_pool(name="sums", bufs=5))
+        work = stack.enter_context(tc.tile_pool(name="work", bufs=4))
+        stats = stack.enter_context(tc.tile_pool(name="stats", bufs=4))
         turn = stack.enter_context(tc.psum_pool(name="turn", bufs=2))
         accs = stack.enter_context(tc.psum_pool(name="accs", bufs=4))
         copies = stack.enter_context(tc.psum_pool(name="copies", bufs=2))
@@ -200,9 +201,25 @@ def tile_swintransformerblock_pb_t_kernel(
                 )
                 kept["acc", h, a] = acc
 
+        def image_stats(h):
+            if ("stats", h // 2) not in kept:
+                t_sum = stats.tile([P, WS], F32)
+                dev_sq = stats.tile([P, WS], F32)
+                std = stats.tile([P, WS], F32)
+                slope = stats.tile([P, WS], F32)
+                level = stats.tile([P, WS], F32)
+                shifted = stats.tile([P, WS], F32)
+                kept["stats", h // 2] = dict(
+                    t_sum=t_sum, dev_sq=dev_sq, std=std, slope=slope, level=level, shifted=shifted
+                )
+            return kept["stats", h // 2]
+
+        def column(h, name, a):
+            slot = first_out_slot(h) + a
+            return image_stats(h)[name][:, slot : slot + 1]
+
         def add_bias(h):
-            t_all = work.tile([P, BLOCKS, C], F32)
-            t_sum = stats.tile([P, BLOCKS], F32)
+            t_all = sums.tile([P, BLOCKS, C], F32)
             for a in range(BLOCKS):
                 nc.vector.scalar_tensor_tensor(
                     out=t_all[:, a, :],
@@ -211,59 +228,60 @@ def tile_swintransformerblock_pb_t_kernel(
                     in1=bias[:],
                     op0=ALU.mult,
                     op1=ALU.add,
-                    accum_out=t_sum[:, a : a + 1],
+                    accum_out=column(h, "t_sum", a),
                 )
             kept["t", h] = t_all
-            kept["t_sum", h] = t_sum
 
         def squared_deviations(h, blocks):
-            if ("dev_sq", h) not in kept:
-                dev_sq = stats.tile([P, BLOCKS], F32)
-                kept["dev_sq", h] = dev_sq
             for a in blocks:
                 squares = stage.tile([P, C], BF16)
                 nc.scalar.activation(
                     out=squares[:],
                     in_=kept["t", h][:, a, :],
                     func=ACT.Square,
-                    bias=kept["t_sum", h][:, a : a + 1],
+                    bias=column(h, "t_sum", a),
                     scale=-1.0 * C,
-                    accum_out=kept["dev_sq", h][:, a : a + 1],
+                    accum_out=column(h, "dev_sq", a),
                 )
 
-        def standard_deviation(h):
-            std = stats.tile([P, BLOCKS], F32)
+        IMAGE = slice(0, WS)
+
+        def standard_deviation(h, cols):
+            st = image_stats(h)
             nc.scalar.activation(
-                out=std[:], in_=kept["dev_sq", h][:], func=ACT.Sqrt, scale=1.0 / ((C - 1) * C * C)
+                out=st["std"][:, cols],
+                in_=st["dev_sq"][:, cols],
+                func=ACT.Sqrt,
+                scale=1.0 / ((C - 1) * C * C),
             )
-            kept["std", h] = std
 
-        def add_eps(h):
-            std = kept["std", h]
-            nc.scalar.add(std[:], std[:], EPS)
+        def add_eps(h, cols):
+            std = image_stats(h)["std"][:, cols]
+            nc.scalar.add(std, std, EPS)
 
-        def slope_step(h, step):
+        def slope_step(h, cols, step):
+            st = image_stats(h)
+            slope = st["slope"][:, cols]
             if step == 0:
-                slope = stats.tile([P, BLOCKS], F32)
-                level = stats.tile([P, BLOCKS], F32)
-                kept["slope", h] = slope
-                kept["level", h] = level
-                nc.vector.reciprocal(out=slope[:], in_=kept["std", h][:])
-            slope = kept["slope", h]
-            level = kept["level", h]
+                nc.vector.reciprocal(out=slope, in_=st["std"][:, cols])
             if step == 1:
-                nc.vector.tensor_mul(out=slope[:], in0=slope[:], in1=gain[:, out_slots(h)])
+                nc.vector.tensor_mul(out=slope, in0=slope, in1=gain[:, cols])
             if step == 2:
                 nc.vector.scalar_tensor_tensor(
-                    out=level[:],
-                    in0=kept["t_sum", h][:],
+                    out=st["level"][:, cols],
+                    in0=st["t_sum"][:, cols],
                     scalar=-1.0 / C,
-                    in1=slope[:],
+                    in1=slope,
                     op0=ALU.mult,
                     op1=ALU.mult,
                 )
-            if step == 3:
-                nc.vector.tensor_add(out=level[:], in0=level[:], in1=offset[:, out_slots(h)])
+
+        def add_offset(h):
+            st = image_stats(h)
+            cols = out_slots(h)
+            nc.vector.tensor_add(
+                out=st["shifted"][:, cols], in0=st["level"][:, cols], in1=offset[:, cols]
+            )
 
         def result_of(h):
             if ("result", h) not in kept:
@@ -277,27 +295,26 @@ def tile_swintransformerblock_pb_t_kernel(
                     out=result_of(h)[:, a, :],
                     in_=kept["t", h][:, a, :],
                     func=ACT.Identity,
-                    bias=kept["level", h][:, a : a + 1],
-                    scale=kept["slope", h][:, a : a + 1],
+                    bias=column(h, "shifted", a),
+                    scale=column(h, "slope", a),
                 )
 
-        def vector_normalise(h, a):
-            nc.vector.tensor_scalar(
-                out=result_of(h)[:, a, :],
-                in0=kept["t", h][:, a, :],
-                scalar1=kept["slope", h][:, a : a + 1],
-                scalar2=kept["level", h][:, a : a + 1],
-                op0=ALU.mult,
-                op1=ALU.add,
-            )
+        def gpsimd_normalise(h):
+            for a in GPSIMD_BLOCKS:
+                nc.gpsimd.tensor_scalar(
+                    out=result_of(h)[:, a, :],
+                    in0=kept["t", h][:, a, :],
+                    scalar1=column(h, "slope", a),
+                    scalar2=column(h, "shifted", a),
+                    op0=ALU.mult,
+                    op1=ALU.add,
+                )
 
-        def gpsimd_add_x(h, blocks):
+        def add_x(engine, h, a):
             result = kept["result", h]
-            nc.gpsimd.tensor_add(
-                out=result[:, blocks, :], in0=result[:, blocks, :], in1=kept["x", h][:, blocks, :]
-            )
+            engine.tensor_add(out=result[:, a, :], in0=result[:, a, :], in1=kept["x", h][:, a, :])
 
-        def vector_add_x(h, blocks):
+        def add_x_by_psum(h, blocks):
             result = kept["result", h]
             for a in blocks:
                 x_bank = copies.tile([P, C], F32)
@@ -322,8 +339,8 @@ def tile_swintransformerblock_pb_t_kernel(
         turn_bank(0, 1)
         group_bank(0, 1, nc.scalar.copy)
         quantise(0, 0)
-        turn_bank(1, 0)
         project(0, 0)
+        turn_bank(1, 0)
         quantise(0, 1)
         group_bank(1, 0, nc.scalar.copy)
         turn_bank(1, 1)
@@ -331,95 +348,82 @@ def tile_swintransformerblock_pb_t_kernel(
         group_bank(1, 1, nc.scalar.copy)
 
         for i in range(FULL_ROUNDS):
+            image_done = i if i % 2 == 0 else -1
             run(load_o, i + O_AHEAD)
             load_x(i)
             run(squared_deviations, i - 1, range(BLOCKS))
             run(turn_bank, i + 2, 0)
             run(group_bank, i + 2, 0, nc.scalar.copy)
-            run(standard_deviation, i - 1)
-            run(scalar_normalise, i - 2, SCALAR_BLOCKS[:1])
-            run(add_eps, i - 1)
-            run(scalar_normalise, i - 2, SCALAR_BLOCKS[1:])
-            if i < 2:
-                run(turn_bank, i + 2, 1)
-                run(group_bank, i + 2, 1, nc.scalar.copy)
-            run(gpsimd_add_x, i - 3, GPSIMD_BLOCKS)
-            for pair in range(PAIRS):
-                run(store, i - 3, 2 * pair, 2)
+            run(standard_deviation, image_done - 1, IMAGE)
+            run(turn_bank, i + 2, 1)
+            run(group_bank, i + 2, 1, nc.scalar.copy)
+            run(add_eps, image_done - 1, IMAGE)
+            run(scalar_normalise, i - 3, SCALAR_BLOCKS)
+            run(gpsimd_normalise, i - 3)
+            if i >= 3:
+                add_x(nc.gpsimd, i - 3, LAST)
             add_bias(i)
-            if i >= 2:
-                run(turn_bank, i + 2, 1)
-                run(group_bank, i + 2, 1, nc.vector.tensor_copy)
-            run(vector_add_x, i - 2, (0,))
-            run(slope_step, i - 1, 0)
+            run(add_x_by_psum, i - 3, (0,))
+            run(slope_step, image_done - 1, IMAGE, 0)
             quantise(i + 1, 0)
-            run(slope_step, i - 1, 1)
+            run(slope_step, image_done - 1, IMAGE, 1)
             quantise(i + 1, 1)
             for pair in range(PAIRS):
                 project(i + 1, pair)
-            run(slope_step, i - 1, 2)
-            run(slope_step, i - 1, 3)
-            run(vector_normalise, i - 2, VECTOR_BLOCK)
+            run(slope_step, image_done - 1, IMAGE, 2)
+            if i >= 3:
+                add_x(nc.vector, i - 3, 1)
+                add_x(nc.vector, i - 3, 2)
+            run(add_offset, i - 2)
+            for pair in range(PAIRS):
+                run(store, i - 3, 2 * pair, 2)
 
         e = halves - 1
-        for h in (e - 1, e):
-            load_x(h)
-        squared_deviations(e - 2, range(BLOCKS))
-        standard_deviation(e - 2)
-        add_eps(e - 2)
-        scalar_normalise(e - 3, SCALAR_BLOCKS)
-        gpsimd_add_x(e - 4, GPSIMD_BLOCKS)
-        store(e - 4, 0, 2)
-        store(e - 4, 2, 2)
-        add_bias(e - 1)
-        vector_add_x(e - 3, (0,))
-        slope_step(e - 2, 0)
-        quantise(e, 0)
-        slope_step(e - 2, 1)
-        quantise(e, 1)
-        for pair in range(PAIRS):
-            project(e, pair)
-        slope_step(e - 2, 2)
-        slope_step(e - 2, 3)
-        vector_normalise(e - 3, VECTOR_BLOCK)
-
+        load_x(e)
+        add_offset(e - 2)
         squared_deviations(e - 1, range(BLOCKS))
-        standard_deviation(e - 1)
-        add_eps(e - 1)
-        gpsimd_add_x(e - 3, GPSIMD_BLOCKS)
-        store(e - 3, 0, 2)
-        store(e - 3, 2, 2)
+        standard_deviation(e - 1, out_slots(e - 1))
+        add_eps(e - 1, out_slots(e - 1))
+        scalar_normalise(e - 3, SCALAR_BLOCKS)
+        gpsimd_normalise(e - 3)
+        add_x(nc.gpsimd, e - 3, LAST)
         add_bias(e)
-        scalar_normalise(e - 2, (0, 1))
+        scalar_normalise(e - 2, (0,))
         squared_deviations(e, (0, 1))
-        scalar_normalise(e - 2, (2,))
+        scalar_normalise(e - 2, (1,))
         squared_deviations(e, (2, 3))
-        standard_deviation(e)
-        add_eps(e)
-        vector_add_x(e - 2, (0, 1))
+        standard_deviation(e, out_slots(e))
+        add_eps(e, out_slots(e))
+        add_x_by_psum(e - 3, (0,))
+        slope_step(e - 1, out_slots(e - 1), 0)
+        add_x(nc.vector, e - 3, 1)
+        store(e - 3, 0, 2)
+        slope_step(e - 1, out_slots(e - 1), 1)
+        add_x(nc.vector, e - 3, 2)
+        store(e - 3, 2, 2)
+        slope_step(e - 1, out_slots(e - 1), 2)
+        add_x_by_psum(e - 2, (0,))
+        add_offset(e - 1)
+        gpsimd_normalise(e - 2)
+        gpsimd_normalise(e - 1)
+        scalar_normalise(e - 1, SCALAR_BLOCKS)
+        add_x_by_psum(e - 2, (1,))
         store(e - 2, 0, 2)
-        slope_step(e - 1, 0)
-        vector_normalise(e - 2, 3)
-        slope_step(e - 1, 1)
-        vector_add_x(e - 2, (2,))
-        slope_step(e - 1, 2)
-        vector_add_x(e - 2, (3,))
-        store(e - 2, 2, 2)
-        slope_step(e - 1, 3)
-        slope_step(e, 0)
-        vector_normalise(e - 1, 2)
-        slope_step(e, 1)
-        vector_normalise(e - 1, 3)
-        slope_step(e, 2)
-        slope_step(e, 3)
-        scalar_normalise(e - 1, (0, 1))
-        gpsimd_add_x(e - 1, slice(0, 2))
+        slope_step(e, out_slots(e), 0)
+        add_x_by_psum(e - 2, (2,))
+        slope_step(e, out_slots(e), 1)
+        add_x_by_psum(e - 1, (0,))
+        slope_step(e, out_slots(e), 2)
+        add_x_by_psum(e - 1, (1,))
         store(e - 1, 0, 2)
-        vector_add_x(e - 1, (2, 3))
+        add_offset(e)
+        add_x(nc.vector, e - 2, LAST)
+        store(e - 2, 2, 2)
+        add_x_by_psum(e - 1, (2, 3))
         store(e - 1, 2, 2)
         scalar_normalise(e, range(BLOCKS))
-        vector_add_x(e, (0, 1))
+        add_x_by_psum(e, (0, 1))
         store(e, 0, 2)
         for a in (2, 3):
-            vector_add_x(e, (a,))
+            add_x_by_psum(e, (a,))
             store(e, a, 1)

@@ -22,10 +22,11 @@ BLOCKS = 4
 PAIRS = BLOCKS // 2
 EPS = 1e-5
 SCALAR_BLOCKS = (0, 1)
-GPSIMD_BLOCKS = (2, 3)
-LAST = BLOCKS - 1
-FULL_ROUNDS = 2 * IMAGES - 1
-O_AHEAD = 3
+VECTOR_BLOCK = 2
+GPSIMD_BLOCK = 3
+FULL_ROUNDS = 2 * IMAGES - 2
+O_AHEAD = 5
+X_AHEAD = 1
 LOAD_BUFS = 7
 
 FLOPS = 2 * IMAGES * GRID * GRID * C * C
@@ -51,7 +52,7 @@ def make_window_permutation(nc, perm, ident, carry):
 
 
 def turn_pair(nc, turn, rows, perm, pair):
-    turned = turn.tile([P, 2, 2, P], F32)
+    turned = turn.tile([P, 2, 2, P], F32, tag="turned")
     for a in range(2):
         words = rows[:, 2 * pair + a, :].bitcast(F32)
         for u in range(2):
@@ -97,11 +98,11 @@ def tile_swintransformerblock_pb_t_kernel(
         loads = stack.enter_context(tc.tile_pool(name="loads", bufs=LOAD_BUFS))
         stage = stack.enter_context(tc.tile_pool(name="stage", bufs=2))
         sums = stack.enter_context(tc.tile_pool(name="sums", bufs=5))
-        work = stack.enter_context(tc.tile_pool(name="work", bufs=4))
+        work = stack.enter_context(tc.tile_pool(name="work", bufs=5))
         stats = stack.enter_context(tc.tile_pool(name="stats", bufs=4))
-        turn = stack.enter_context(tc.psum_pool(name="turn", bufs=2))
+        turn = stack.enter_context(tc.psum_pool(name="turn", bufs=3))
         accs = stack.enter_context(tc.psum_pool(name="accs", bufs=4))
-        copies = stack.enter_context(tc.psum_pool(name="copies", bufs=2))
+        copies = stack.enter_context(tc.psum_pool(name="copies", bufs=1))
         stack.enter_context(tc.manual_schedule())
 
         kept = {}
@@ -131,6 +132,8 @@ def tile_swintransformerblock_pb_t_kernel(
             nc.sync.dma_start(out=w_rows[:, a : a + 2, :], in_=w_view[:, a : a + 2, :])
         for h in range(O_AHEAD):
             load_o(h)
+        for h in range(X_AHEAD):
+            load_x(h)
         gain = consts.tile([P, WS], BF16)
         nc.sync.dma_start(
             out=gain[:], in_=ada1_scale.flatten_outer_dims().rearrange("(p s) q -> p (s q)", p=P)
@@ -172,11 +175,11 @@ def tile_swintransformerblock_pb_t_kernel(
         def turn_bank(h, pair):
             kept["bank", h, pair] = turn_pair(nc, turn, kept["o", h], perms[h % 2][:], pair)
 
-        def group_bank(h, pair, copy_out):
+        def group_bank(h, pair):
             if pair == 0:
                 grouped = stage.tile([P, BLOCKS * C], BF16, align_bytes=64, tag="grouped")
                 kept["grouped", h] = grouped
-            group_words(copy_out, kept["grouped", h], kept["bank", h, pair], pair)
+            group_words(nc.scalar.copy, kept["grouped", h], kept["bank", h, pair], pair)
 
         def quantise(h, pair):
             if pair == 0:
@@ -218,11 +221,13 @@ def tile_swintransformerblock_pb_t_kernel(
             slot = first_out_slot(h) + a
             return image_stats(h)[name][:, slot : slot + 1]
 
-        def add_bias(h):
-            t_all = sums.tile([P, BLOCKS, C], F32)
-            for a in range(BLOCKS):
+        def add_bias(h, blocks):
+            if ("t", h) not in kept:
+                t_all = sums.tile([P, BLOCKS, C], F32)
+                kept["t", h] = t_all
+            for a in blocks:
                 nc.vector.scalar_tensor_tensor(
-                    out=t_all[:, a, :],
+                    out=kept["t", h][:, a, :],
                     in0=kept["acc", h, a][:],
                     scalar=1.0,
                     in1=bias[:],
@@ -230,7 +235,6 @@ def tile_swintransformerblock_pb_t_kernel(
                     op1=ALU.add,
                     accum_out=column(h, "t_sum", a),
                 )
-            kept["t", h] = t_all
 
         def squared_deviations(h, blocks):
             for a in blocks:
@@ -299,29 +303,37 @@ def tile_swintransformerblock_pb_t_kernel(
                     scale=column(h, "slope", a),
                 )
 
-        def gpsimd_normalise(h):
-            for a in GPSIMD_BLOCKS:
-                nc.gpsimd.tensor_scalar(
-                    out=result_of(h)[:, a, :],
-                    in0=kept["t", h][:, a, :],
-                    scalar1=column(h, "slope", a),
-                    scalar2=column(h, "shifted", a),
-                    op0=ALU.mult,
-                    op1=ALU.add,
-                )
+        def normalise(engine, h, a):
+            engine.tensor_scalar(
+                out=result_of(h)[:, a, :],
+                in0=kept["t", h][:, a, :],
+                scalar1=column(h, "slope", a),
+                scalar2=column(h, "shifted", a),
+                op0=ALU.mult,
+                op1=ALU.add,
+            )
 
-        def add_x(engine, h, a):
+        def add_x(engine, h, blocks):
             result = kept["result", h]
-            engine.tensor_add(out=result[:, a, :], in0=result[:, a, :], in1=kept["x", h][:, a, :])
+            engine.tensor_add(
+                out=result[:, blocks, :], in0=result[:, blocks, :], in1=kept["x", h][:, blocks, :]
+            )
+
+        def copy_x(h, a, pool, tag):
+            x_bank = pool.tile([P, C], F32, tag=tag)
+            nc.tensor.matmul(
+                x_bank[:], lhsT=ident_bf16[:], rhs=kept["x", h][:, a, :], start=True, stop=True
+            )
+            kept["x_bank", h, a] = x_bank
+
+        def add_copied_x(h, a):
+            result = kept["result", h]
+            nc.vector.tensor_add(out=result[:, a, :], in0=result[:, a, :], in1=kept["x_bank", h, a][:])
 
         def add_x_by_psum(h, blocks):
-            result = kept["result", h]
             for a in blocks:
-                x_bank = copies.tile([P, C], F32)
-                nc.tensor.matmul(
-                    x_bank[:], lhsT=ident_bf16[:], rhs=kept["x", h][:, a, :], start=True, stop=True
-                )
-                nc.vector.tensor_add(out=result[:, a, :], in0=result[:, a, :], in1=x_bank[:])
+                copy_x(h, a, turn, "turned")
+                add_copied_x(h, a)
 
         def store(h, first, count):
             slot = first_out_slot(h) + first
@@ -335,95 +347,124 @@ def tile_swintransformerblock_pb_t_kernel(
                 stage_of_half(h, *more)
 
         turn_bank(0, 0)
-        group_bank(0, 0, nc.scalar.copy)
+        group_bank(0, 0)
         turn_bank(0, 1)
-        group_bank(0, 1, nc.scalar.copy)
+        group_bank(0, 1)
         quantise(0, 0)
         project(0, 0)
-        turn_bank(1, 0)
         quantise(0, 1)
-        group_bank(1, 0, nc.scalar.copy)
-        turn_bank(1, 1)
+        turn_bank(1, 0)
+        group_bank(1, 0)
         project(0, 1)
-        group_bank(1, 1, nc.scalar.copy)
+        turn_bank(1, 1)
+        group_bank(1, 1)
 
         for i in range(FULL_ROUNDS):
-            image_done = i if i % 2 == 0 else -1
+            whole = i - 1 if i % 2 == 0 else -1
             run(load_o, i + O_AHEAD)
-            load_x(i)
+            load_x(i + X_AHEAD)
             run(squared_deviations, i - 1, range(BLOCKS))
+            if i > 0:
+                group_bank(i + 1, 0)
             run(turn_bank, i + 2, 0)
-            run(group_bank, i + 2, 0, nc.scalar.copy)
-            run(standard_deviation, image_done - 1, IMAGE)
+            run(standard_deviation, whole, IMAGE)
+            if i > 0:
+                group_bank(i + 1, 1)
             run(turn_bank, i + 2, 1)
-            run(group_bank, i + 2, 1, nc.scalar.copy)
-            run(add_eps, image_done - 1, IMAGE)
+            run(add_eps, whole, IMAGE)
             run(scalar_normalise, i - 3, SCALAR_BLOCKS)
-            run(gpsimd_normalise, i - 3)
+            run(copy_x, i - 3, 1, copies, "x_bank")
+            add_bias(i, (0, 1))
+            run(slope_step, whole, IMAGE, 0)
+            add_bias(i, (2, 3))
+            run(slope_step, whole, IMAGE, 1)
             if i >= 3:
-                add_x(nc.gpsimd, i - 3, LAST)
-            add_bias(i)
-            run(add_x_by_psum, i - 3, (0,))
-            run(slope_step, image_done - 1, IMAGE, 0)
+                add_x(nc.vector, i - 3, slice(0, 1))
+            run(slope_step, whole, IMAGE, 2)
             quantise(i + 1, 0)
-            run(slope_step, image_done - 1, IMAGE, 1)
             quantise(i + 1, 1)
             for pair in range(PAIRS):
                 project(i + 1, pair)
-            run(slope_step, image_done - 1, IMAGE, 2)
-            if i >= 3:
-                add_x(nc.vector, i - 3, 1)
-                add_x(nc.vector, i - 3, 2)
             run(add_offset, i - 2)
-            for pair in range(PAIRS):
-                run(store, i - 3, 2 * pair, 2)
+            if i >= 3:
+                normalise(nc.vector, i - 3, VECTOR_BLOCK)
+                add_copied_x(i - 3, 1)
+            if i >= 2:
+                normalise(nc.gpsimd, i - 2, GPSIMD_BLOCK)
+            if i >= 3:
+                add_x(nc.gpsimd, i - 3, slice(2, 4))
+                store(i - 3, 0, 2)
+                store(i - 3, 2, 2)
 
         e = halves - 1
         load_x(e)
-        add_offset(e - 2)
+        squared_deviations(e - 2, range(BLOCKS))
+        group_bank(e, 0)
+        standard_deviation(e - 2, IMAGE)
+        group_bank(e, 1)
+        add_eps(e - 2, IMAGE)
+        scalar_normalise(e - 4, SCALAR_BLOCKS)
+        copy_x(e - 4, 1, copies, "x_bank")
+        add_bias(e - 1, (0, 1))
+        slope_step(e - 2, IMAGE, 0)
+        add_bias(e - 1, (2, 3))
         squared_deviations(e - 1, range(BLOCKS))
         standard_deviation(e - 1, out_slots(e - 1))
         add_eps(e - 1, out_slots(e - 1))
-        scalar_normalise(e - 3, SCALAR_BLOCKS)
-        gpsimd_normalise(e - 3)
-        add_x(nc.gpsimd, e - 3, LAST)
-        add_bias(e)
-        scalar_normalise(e - 2, (0,))
-        squared_deviations(e, (0, 1))
-        scalar_normalise(e - 2, (1,))
+        slope_step(e - 2, IMAGE, 1)
+        add_x(nc.vector, e - 4, slice(0, 1))
+        slope_step(e - 2, IMAGE, 2)
+        quantise(e, 0)
+        quantise(e, 1)
+        for pair in range(PAIRS):
+            project(e, pair)
+        slope_step(e - 1, out_slots(e - 1), 0)
+        add_offset(e - 2)
+        normalise(nc.vector, e - 4, VECTOR_BLOCK)
+        slope_step(e - 1, out_slots(e - 1), 1)
+        slope_step(e - 1, out_slots(e - 1), 2)
+        add_offset(e - 3)
+        add_offset(e - 1)
+        add_copied_x(e - 4, 1)
+        for a in (3, 2):
+            normalise(nc.gpsimd, e - 3, a)
+        add_x(nc.gpsimd, e - 4, slice(2, 4))
+        store(e - 4, 0, 2)
+        store(e - 4, 2, 2)
+
+        scalar_normalise(e - 3, (0, 1))
+        add_bias(e, range(BLOCKS))
+        for a in (0, 1):
+            squared_deviations(e, (a,))
+            scalar_normalise(e - 2, (a,))
         squared_deviations(e, (2, 3))
         standard_deviation(e, out_slots(e))
         add_eps(e, out_slots(e))
-        add_x_by_psum(e - 3, (0,))
-        slope_step(e - 1, out_slots(e - 1), 0)
-        add_x(nc.vector, e - 3, 1)
+        scalar_normalise(e - 2, (2, 3))
+        add_x(nc.gpsimd, e - 3, slice(2, 4))
+        add_x_by_psum(e - 3, (0, 1))
         store(e - 3, 0, 2)
-        slope_step(e - 1, out_slots(e - 1), 1)
-        add_x(nc.vector, e - 3, 2)
         store(e - 3, 2, 2)
-        slope_step(e - 1, out_slots(e - 1), 2)
-        add_x_by_psum(e - 2, (0,))
-        add_offset(e - 1)
-        gpsimd_normalise(e - 2)
-        gpsimd_normalise(e - 1)
-        scalar_normalise(e - 1, SCALAR_BLOCKS)
-        add_x_by_psum(e - 2, (1,))
+        add_x_by_psum(e - 2, (0, 1))
         store(e - 2, 0, 2)
         slope_step(e, out_slots(e), 0)
-        add_x_by_psum(e - 2, (2,))
+        add_x_by_psum(e - 2, (2, 3))
+        store(e - 2, 2, 2)
+        scalar_normalise(e - 1, (0, 1))
+        for a in (2, 3):
+            normalise(nc.gpsimd, e - 1, a)
         slope_step(e, out_slots(e), 1)
         add_x_by_psum(e - 1, (0,))
         slope_step(e, out_slots(e), 2)
         add_x_by_psum(e - 1, (1,))
         store(e - 1, 0, 2)
         add_offset(e)
-        add_x(nc.vector, e - 2, LAST)
-        store(e - 2, 2, 2)
-        add_x_by_psum(e - 1, (2, 3))
+        scalar_normalise(e, (0, 1, 2))
+        for a in (2, 3):
+            add_x(nc.vector, e - 1, slice(a, a + 1))
         store(e - 1, 2, 2)
-        scalar_normalise(e, range(BLOCKS))
+        normalise(nc.vector, e, 3)
         add_x_by_psum(e, (0, 1))
         store(e, 0, 2)
-        for a in (2, 3):
-            add_x_by_psum(e, (a,))
-            store(e, a, 1)
+        add_x_by_psum(e, (3, 2))
+        store(e, 2, 2)

@@ -25,9 +25,7 @@ SCALAR_BLOCKS = (0, 1)
 VECTOR_BLOCK = 2
 GPSIMD_BLOCK = 3
 FULL_ROUNDS = 2 * IMAGES - 2
-O_AHEAD = 5
-X_AHEAD = 1
-LOAD_BUFS = 7
+LOADS_AHEAD = 4
 
 FLOPS = 2 * IMAGES * GRID * GRID * C * C
 
@@ -95,7 +93,7 @@ def tile_swintransformerblock_pb_t_kernel(
 
     with ExitStack() as stack:
         consts = stack.enter_context(tc.tile_pool(name="consts", bufs=1))
-        loads = stack.enter_context(tc.tile_pool(name="loads", bufs=LOAD_BUFS))
+        loads = stack.enter_context(tc.tile_pool(name="loads", bufs=IMAGES - 1))
         stage = stack.enter_context(tc.tile_pool(name="stage", bufs=2))
         sums = stack.enter_context(tc.tile_pool(name="sums", bufs=5))
         work = stack.enter_context(tc.tile_pool(name="work", bufs=5))
@@ -107,21 +105,22 @@ def tile_swintransformerblock_pb_t_kernel(
 
         kept = {}
 
-        def load_o(h):
-            o_tile = loads.tile([P, BLOCKS, C], BF16)
-            first = BLOCKS * (h % 2)
-            step = 2 if h == 0 else BLOCKS
-            for a in range(0, BLOCKS, step):
-                nc.sync.dma_start(
-                    out=o_tile[:, a : a + step, :],
-                    in_=o_rows[h // 2, :, first + a : first + a + step, :],
-                )
-            kept["o", h] = o_tile
+        def load_o(b):
+            o_tile = loads.tile([P, WS, C], BF16)
+            pieces = (2, 2, 4) if b == 0 else (WS,)
+            first = 0
+            for count in pieces:
+                slots = slice(first, first + count)
+                nc.sync.dma_start(out=o_tile[:, slots, :], in_=o_rows[b, :, slots, :])
+                first += count
+            for half in range(2):
+                kept["o", 2 * b + half] = o_tile[:, half * BLOCKS : (half + 1) * BLOCKS, :]
 
-        def load_x(h):
-            x_tile = loads.tile([P, BLOCKS, C], BF16)
-            nc.sync.dma_start(out=x_tile[:], in_=x_rows[h // 2, :, out_slots(h), :])
-            kept["x", h] = x_tile
+        def load_x(b):
+            x_tile = loads.tile([P, WS, C], BF16)
+            nc.sync.dma_start(out=x_tile[:], in_=x_rows[b])
+            for h in (2 * b, 2 * b + 1):
+                kept["x", h] = x_tile[:, out_slots(h), :]
 
         bias_row = consts.tile([P, C], BF16)
         nc.vector.memset(bias_row[:], 0.0)
@@ -130,10 +129,8 @@ def tile_swintransformerblock_pb_t_kernel(
         w_view = out_w.rearrange("(a p) k -> p a k", p=P)
         for a in range(0, BLOCKS, 2):
             nc.sync.dma_start(out=w_rows[:, a : a + 2, :], in_=w_view[:, a : a + 2, :])
-        for h in range(O_AHEAD):
-            load_o(h)
-        for h in range(X_AHEAD):
-            load_x(h)
+        load_o(0)
+        load_o(1)
         gain = consts.tile([P, WS], BF16)
         nc.sync.dma_start(
             out=gain[:], in_=ada1_scale.flatten_outer_dims().rearrange("(p s) q -> p (s q)", p=P)
@@ -142,6 +139,12 @@ def tile_swintransformerblock_pb_t_kernel(
         nc.sync.dma_start(
             out=offset[:], in_=ada1_shift.flatten_outer_dims().rearrange("(p s) q -> p (s q)", p=P)
         )
+
+        order = [load for b in range(IMAGES) for load in ((load_x, b), (load_o, b + 2))][:-4]
+        order += [(load_x, IMAGES - 2), (load_x, IMAGES - 1)]
+        for load, b in order[:LOADS_AHEAD]:
+            load(b)
+        later_loads = order[LOADS_AHEAD:]
 
         ones = consts.tile([P, P], BF16)
         nc.vector.memset(ones[:], 1.0)
@@ -361,8 +364,8 @@ def tile_swintransformerblock_pb_t_kernel(
 
         for i in range(FULL_ROUNDS):
             whole = i - 1 if i % 2 == 0 else -1
-            run(load_o, i + O_AHEAD)
-            load_x(i + X_AHEAD)
+            for load, b in later_loads[i : i + 1]:
+                load(b)
             run(squared_deviations, i - 1, range(BLOCKS))
             if i > 0:
                 group_bank(i + 1, 0)
@@ -393,11 +396,9 @@ def tile_swintransformerblock_pb_t_kernel(
                 normalise(nc.gpsimd, i - 2, GPSIMD_BLOCK)
             if i >= 3:
                 add_x(nc.gpsimd, i - 3, slice(2, 4))
-                store(i - 3, 0, 2)
-                store(i - 3, 2, 2)
+                store(i - 3, 0, BLOCKS)
 
         e = halves - 1
-        load_x(e)
         squared_deviations(e - 2, range(BLOCKS))
         group_bank(e, 0)
         standard_deviation(e - 2, IMAGE)

@@ -24,7 +24,7 @@ EPS = 1e-5
 SCALAR_BLOCKS = (0, 1)
 VECTOR_BLOCK = 2
 GPSIMD_BLOCK = 3
-FULL_ROUNDS = 2 * IMAGES - 2
+ROUNDS = range(1, 2 * IMAGES - 1)
 LOADS_AHEAD = 4
 
 FLOPS = 2 * IMAGES * GRID * GRID * C * C
@@ -353,26 +353,34 @@ def tile_swintransformerblock_pb_t_kernel(
         group_bank(0, 0)
         turn_bank(0, 1)
         group_bank(0, 1)
-        quantise(0, 0)
-        project(0, 0)
-        quantise(0, 1)
         turn_bank(1, 0)
-        group_bank(1, 0)
-        project(0, 1)
+        for pair in range(PAIRS):
+            quantise(0, pair)
+            project(0, pair)
         turn_bank(1, 1)
+        group_bank(1, 0)
+        add_bias(0, (0, 1))
+        squared_deviations(0, (0, 1))
         group_bank(1, 1)
+        add_bias(0, (2, 3))
+        squared_deviations(0, (2, 3))
+        turn_bank(2, 0)
+        turn_bank(2, 1)
+        for pair in range(PAIRS):
+            quantise(1, pair)
+        for pair in range(PAIRS):
+            project(1, pair)
 
-        for i in range(FULL_ROUNDS):
+        for i in ROUNDS:
             whole = i - 1 if i % 2 == 0 else -1
-            for load, b in later_loads[i : i + 1]:
+            for load, b in later_loads[i - 1 : i]:
                 load(b)
-            run(squared_deviations, i - 1, range(BLOCKS))
-            if i > 0:
-                group_bank(i + 1, 0)
+            if i > 1:
+                squared_deviations(i - 1, range(BLOCKS))
+            group_bank(i + 1, 0)
             run(turn_bank, i + 2, 0)
             run(standard_deviation, whole, IMAGE)
-            if i > 0:
-                group_bank(i + 1, 1)
+            group_bank(i + 1, 1)
             run(turn_bank, i + 2, 1)
             run(add_eps, whole, IMAGE)
             run(scalar_normalise, i - 3, SCALAR_BLOCKS)
@@ -384,10 +392,12 @@ def tile_swintransformerblock_pb_t_kernel(
             if i >= 3:
                 add_x(nc.vector, i - 3, slice(0, 1))
             run(slope_step, whole, IMAGE, 2)
-            quantise(i + 1, 0)
-            quantise(i + 1, 1)
+            for pair in range(PAIRS):
+                quantise(i + 1, pair)
             for pair in range(PAIRS):
                 project(i + 1, pair)
+            if i == ROUNDS[-1]:
+                add_offset(i - 1)
             run(add_offset, i - 2)
             if i >= 3:
                 normalise(nc.vector, i - 3, VECTOR_BLOCK)
@@ -399,73 +409,43 @@ def tile_swintransformerblock_pb_t_kernel(
                 store(i - 3, 0, BLOCKS)
 
         e = halves - 1
-        squared_deviations(e - 2, range(BLOCKS))
-        group_bank(e, 0)
-        standard_deviation(e - 2, IMAGE)
-        group_bank(e, 1)
-        add_eps(e - 2, IMAGE)
-        scalar_normalise(e - 4, SCALAR_BLOCKS)
-        copy_x(e - 4, 1, copies, "x_bank")
-        add_bias(e - 1, (0, 1))
-        slope_step(e - 2, IMAGE, 0)
-        add_bias(e - 1, (2, 3))
         squared_deviations(e - 1, range(BLOCKS))
-        standard_deviation(e - 1, out_slots(e - 1))
-        add_eps(e - 1, out_slots(e - 1))
-        slope_step(e - 2, IMAGE, 1)
-        add_x(nc.vector, e - 4, slice(0, 1))
-        slope_step(e - 2, IMAGE, 2)
-        quantise(e, 0)
-        quantise(e, 1)
-        for pair in range(PAIRS):
-            project(e, pair)
-        slope_step(e - 1, out_slots(e - 1), 0)
-        add_offset(e - 2)
-        normalise(nc.vector, e - 4, VECTOR_BLOCK)
-        slope_step(e - 1, out_slots(e - 1), 1)
-        slope_step(e - 1, out_slots(e - 1), 2)
-        add_offset(e - 3)
-        add_offset(e - 1)
-        add_copied_x(e - 4, 1)
-        for a in (3, 2):
-            normalise(nc.gpsimd, e - 3, a)
-        add_x(nc.gpsimd, e - 4, slice(2, 4))
-        store(e - 4, 0, 2)
-        store(e - 4, 2, 2)
-
-        scalar_normalise(e - 3, (0, 1))
+        scalar_normalise(e - 3, (0, 1, 2))
         add_bias(e, range(BLOCKS))
         for a in (0, 1):
             squared_deviations(e, (a,))
             scalar_normalise(e - 2, (a,))
         squared_deviations(e, (2, 3))
-        standard_deviation(e, out_slots(e))
-        add_eps(e, out_slots(e))
-        scalar_normalise(e - 2, (2, 3))
+        standard_deviation(e, IMAGE)
+        add_eps(e, IMAGE)
         add_x(nc.gpsimd, e - 3, slice(2, 4))
         add_x_by_psum(e - 3, (0, 1))
         store(e - 3, 0, 2)
         store(e - 3, 2, 2)
+        for a in (2, 3):
+            normalise(nc.gpsimd, e - 2, a)
         add_x_by_psum(e - 2, (0, 1))
         store(e - 2, 0, 2)
-        slope_step(e, out_slots(e), 0)
-        add_x_by_psum(e - 2, (2, 3))
+        slope_step(e, IMAGE, 0)
+        add_x_by_psum(e - 2, (2,))
+        slope_step(e, IMAGE, 1)
+        add_x_by_psum(e - 2, (3,))
+        slope_step(e, IMAGE, 2)
         store(e - 2, 2, 2)
+        add_offset(e - 1)
+        add_offset(e)
         scalar_normalise(e - 1, (0, 1))
-        for a in (2, 3):
-            normalise(nc.gpsimd, e - 1, a)
-        slope_step(e, out_slots(e), 1)
-        add_x_by_psum(e - 1, (0,))
-        slope_step(e, out_slots(e), 2)
+        normalise(nc.vector, e - 1, 2)
+        normalise(nc.gpsimd, e - 1, 3)
+        normalise(nc.vector, e, 3)
+        add_x_by_psum(e - 1, (2, 0))
+        add_x(nc.vector, e - 1, slice(3, 4))
+        store(e - 1, 2, 2)
         add_x_by_psum(e - 1, (1,))
         store(e - 1, 0, 2)
-        add_offset(e)
         scalar_normalise(e, (0, 1, 2))
-        for a in (2, 3):
-            add_x(nc.vector, e - 1, slice(a, a + 1))
-        store(e - 1, 2, 2)
-        normalise(nc.vector, e, 3)
+        add_x(nc.vector, e, slice(3, 4))
         add_x_by_psum(e, (0, 1))
         store(e, 0, 2)
-        add_x_by_psum(e, (3, 2))
+        add_x_by_psum(e, (2,))
         store(e, 2, 2)

@@ -385,15 +385,14 @@ def tile_swintransformerblock_pb_t_kernel(
             run(add_eps, whole, IMAGE)
             run(scalar_normalise, i - 3, SCALAR_BLOCKS)
             run(copy_x, i - 3, 1, copies, "x_bank")
-            add_bias(i, (0, 1))
+            add_bias(i, range(BLOCKS))
             run(slope_step, whole, IMAGE, 0)
-            add_bias(i, (2, 3))
+            quantise(i + 1, 0)
             run(slope_step, whole, IMAGE, 1)
             if i >= 3:
                 add_x(nc.vector, i - 3, slice(0, 1))
             run(slope_step, whole, IMAGE, 2)
-            for pair in range(PAIRS):
-                quantise(i + 1, pair)
+            quantise(i + 1, 1)
             for pair in range(PAIRS):
                 project(i + 1, pair)
             if i == ROUNDS[-1]:
@@ -412,40 +411,35 @@ def tile_swintransformerblock_pb_t_kernel(
         squared_deviations(e - 1, range(BLOCKS))
         scalar_normalise(e - 3, (0, 1, 2))
         add_bias(e, range(BLOCKS))
-        for a in (0, 1):
-            squared_deviations(e, (a,))
-            scalar_normalise(e - 2, (a,))
-        squared_deviations(e, (2, 3))
+        for a in range(BLOCKS):
+            normalise(nc.gpsimd, e - 2, a)
+        squared_deviations(e, range(BLOCKS))
         standard_deviation(e, IMAGE)
         add_eps(e, IMAGE)
-        add_x(nc.gpsimd, e - 3, slice(2, 4))
-        add_x_by_psum(e - 3, (0, 1))
-        store(e - 3, 0, 2)
-        store(e - 3, 2, 2)
-        for a in (2, 3):
-            normalise(nc.gpsimd, e - 2, a)
+        for first in (0, 2):
+            add_x_by_psum(e - 3, (first, first + 1))
+            store(e - 3, first, 2)
         add_x_by_psum(e - 2, (0, 1))
         store(e - 2, 0, 2)
         slope_step(e, IMAGE, 0)
         add_x_by_psum(e - 2, (2,))
         slope_step(e, IMAGE, 1)
-        add_x_by_psum(e - 2, (3,))
         slope_step(e, IMAGE, 2)
-        store(e - 2, 2, 2)
         add_offset(e - 1)
         add_offset(e)
+        add_x_by_psum(e - 2, (3,))
+        store(e - 2, 2, 2)
         scalar_normalise(e - 1, (0, 1))
-        normalise(nc.vector, e - 1, 2)
-        normalise(nc.gpsimd, e - 1, 3)
-        normalise(nc.vector, e, 3)
-        add_x_by_psum(e - 1, (2, 0))
-        add_x(nc.vector, e - 1, slice(3, 4))
+        for a in (2, 3):
+            normalise(nc.gpsimd, e - 1, a)
+        scalar_normalise(e, (0, 1))
+        add_x_by_psum(e - 1, (2, 0, 3))
         store(e - 1, 2, 2)
         add_x_by_psum(e - 1, (1,))
         store(e - 1, 0, 2)
-        scalar_normalise(e, (0, 1, 2))
-        add_x(nc.vector, e, slice(3, 4))
-        add_x_by_psum(e, (0, 1))
-        store(e, 0, 2)
-        add_x_by_psum(e, (2,))
-        store(e, 2, 2)
+        for a in (2, 3):
+            normalise(nc.vector, e, a)
+        for first in (2, 0):
+            for a in (first, first + 1):
+                add_x(nc.vector, e, slice(a, a + 1))
+            store(e, first, 2)

from contextlib import ExitStack

import concourse.mybir as mybir
from concourse.masks import make_identity

F32 = mybir.dt.float32
BF16 = mybir.dt.bfloat16
U32 = mybir.dt.uint32
U8 = mybir.dt.uint8
FP8X4 = mybir.dt.float8_e4m3fn_x4
ALU = mybir.AluOpType
ACT = mybir.ActivationFunctionType

P = 128
C = 512
IMAGES = 8
GRID = 32
WS = 8
NWIN = GRID // WS
SHIFT = 4
BLOCKS = 4
PAIRS = BLOCKS // 2
EPS = 1e-5
SCALAR_BLOCKS = (0, 1)
VECTOR_BLOCK = 2
GPSIMD_BLOCK = 3
ROUNDS = range(1, 2 * IMAGES - 1)
LOADS_AHEAD = 4

FLOPS = 2 * IMAGES * GRID * GRID * C * C


def rolled(count, shift):
    pieces = [(0, shift, count - shift)]
    if shift:
        pieces.append((count - shift, 0, shift))
    return pieces


def make_window_permutation(nc, perm, ident, carry):
    dst = perm.rearrange("p (wi rh rl wj) -> p wi rh rl wj", wi=NWIN, rh=2, rl=SHIFT, wj=NWIN)
    src = ident.rearrange("p (wi wj rh rl) -> p wi rh rl wj", wi=NWIN, wj=NWIN, rh=2, rl=SHIFT)
    for rh in range(2):
        for wi_src, wi_dst, wi_len in rolled(NWIN, rh):
            for wj_src, wj_dst, wj_len in rolled(NWIN, carry):
                nc.vector.tensor_copy(
                    out=dst[:, wi_dst : wi_dst + wi_len, 1 - rh, :, wj_dst : wj_dst + wj_len],
                    in_=src[:, wi_src : wi_src + wi_len, rh, :, wj_src : wj_src + wj_len],
                )


def turn_pair(nc, turn, rows, perm, pair):
    turned = turn.tile([P, 2, 2, P], F32, tag="turned")
    for a in range(2):
        words = rows[:, 2 * pair + a, :].bitcast(F32)
        for u in range(2):
            nc.tensor.transpose(turned[:, a, u, :], words[:, u : 2 * P : 2], perm)
    return turned


def group_words(copy_out, grouped, bank, pair):
    grouped_words = grouped[:].bitcast(F32).rearrange("p (a j u) -> p a j u", a=BLOCKS, u=2)
    copy_out(
        out=grouped_words[:, 2 * pair : 2 * pair + 2, :, :],
        in_=bank[:].rearrange("p a u j -> p a j u"),
    )


def quantise_pair(nc, grouped, codes, scales, pair):
    cols = slice(2 * P * pair, 2 * P * (pair + 1))
    nc.vector.quantize_mx(
        out=codes[:, cols].bitcast(FP8X4),
        scales=scales[:, cols],
        in_=grouped[:, 2 * C * pair : 2 * C * (pair + 1)],
    )


def tile_swintransformerblock_pb_t_kernel(
    tc, o_attn, out_w, out_b, ada1_scale, ada1_shift, x, out
):
    nc = tc.nc
    halves = 2 * IMAGES

    o_rows = o_attn.flatten_outer_dims().rearrange("(b p c) k -> b p c k", p=P, c=WS)
    x_rows = x.rearrange("b (p s) n -> b p s n", s=WS)
    out_rows = out.rearrange("b (p s) n -> b p s n", s=WS)

    def first_out_slot(h):
        return BLOCKS * (1 - h % 2)

    def out_slots(h):
        return slice(first_out_slot(h), first_out_slot(h) + BLOCKS)

    with ExitStack() as stack:
        consts = stack.enter_context(tc.tile_pool(name="consts", bufs=1))
        loads = stack.enter_context(tc.tile_pool(name="loads", bufs=IMAGES - 1))
        stage = stack.enter_context(tc.tile_pool(name="stage", bufs=2))
        sums = stack.enter_context(tc.tile_pool(name="sums", bufs=5))
        work = stack.enter_context(tc.tile_pool(name="work", bufs=5))
        stats = stack.enter_context(tc.tile_pool(name="stats", bufs=4))
        turn = stack.enter_context(tc.psum_pool(name="turn", bufs=3))
        accs = stack.enter_context(tc.psum_pool(name="accs", bufs=4))
        copies = stack.enter_context(tc.psum_pool(name="copies", bufs=1))
        stack.enter_context(tc.manual_schedule())

        kept = {}

        def load_o(b):
            o_tile = loads.tile([P, WS, C], BF16)
            pieces = (2, 2, 4) if b == 0 else (WS,)
            first = 0
            for count in pieces:
                slots = slice(first, first + count)
                nc.sync.dma_start(out=o_tile[:, slots, :], in_=o_rows[b, :, slots, :])
                first += count
            for half in range(2):
                kept["o", 2 * b + half] = o_tile[:, half * BLOCKS : (half + 1) * BLOCKS, :]

        def load_x(b):
            x_tile = loads.tile([P, WS, C], BF16)
            nc.sync.dma_start(out=x_tile[:], in_=x_rows[b])
            for h in (2 * b, 2 * b + 1):
                kept["x", h] = x_tile[:, out_slots(h), :]

        bias_row = consts.tile([P, C], BF16)
        nc.vector.memset(bias_row[:], 0.0)
        nc.sync.dma_start(out=bias_row[0:1, :], in_=out_b.rearrange("(o n) -> o n", o=1))
        w_rows = consts.tile([P, BLOCKS, C], BF16)
        w_view = out_w.rearrange("(a p) k -> p a k", p=P)
        for a in range(0, BLOCKS, 2):
            nc.sync.dma_start(out=w_rows[:, a : a + 2, :], in_=w_view[:, a : a + 2, :])
        load_o(0)
        load_o(1)
        gain = consts.tile([P, WS], BF16)
        nc.sync.dma_start(
            out=gain[:], in_=ada1_scale.flatten_outer_dims().rearrange("(p s) q -> p (s q)", p=P)
        )
        offset = consts.tile([P, WS], BF16)
        nc.sync.dma_start(
            out=offset[:], in_=ada1_shift.flatten_outer_dims().rearrange("(p s) q -> p (s q)", p=P)
        )

        order = [load for b in range(IMAGES) for load in ((load_x, b), (load_o, b + 2))][:-4]
        order += [(load_x, IMAGES - 2), (load_x, IMAGES - 1)]
        for load, b in order[:LOADS_AHEAD]:
            load(b)
        later_loads = order[LOADS_AHEAD:]

        ones = consts.tile([P, P], BF16)
        nc.vector.memset(ones[:], 1.0)
        table_warmer = consts.tile([P, 1], F32)
        nc.scalar.activation(out=table_warmer[:], in_=ones[:, 0:1], func=ACT.Sqrt)

        ident = consts.tile([P, P], F32)
        make_identity(nc, ident[:])
        ident_bf16 = consts.tile([P, P], BF16)
        perms = []
        for carry in range(2):
            perm = consts.tile([P, P], F32, name="perm%d" % carry)
            make_window_permutation(nc, perm[:], ident[:], carry)
            perms.append(perm)
        nc.vector.tensor_copy(out=ident_bf16[:], in_=ident[:])

        bias_bank = accs.tile([P, C], F32, tag="acc")
        nc.tensor.matmul(bias_bank[:], lhsT=ones[:], rhs=bias_row[:], start=True, stop=True)
        bias = consts.tile([P, C], F32)
        nc.vector.tensor_copy(out=bias[:], in_=bias_bank[:])

        w_codes = consts.tile([P, C], U32, align_bytes=64)
        w_scales = consts.tile([P, C], U8, align_bytes=64)
        w_grouped = stage.tile([P, BLOCKS * C], BF16, align_bytes=64, tag="grouped")
        for pair, copy_out in enumerate((nc.vector.tensor_copy, nc.scalar.copy)):
            w_bank = turn_pair(nc, turn, w_rows, ident[:], pair)
            group_words(copy_out, w_grouped, w_bank, pair)
        for pair in range(PAIRS):
            quantise_pair(nc, w_grouped, w_codes, w_scales, pair)

        def turn_bank(h, pair):
            kept["bank", h, pair] = turn_pair(nc, turn, kept["o", h], perms[h % 2][:], pair)

        def group_bank(h, pair):
            if pair == 0:
                grouped = stage.tile([P, BLOCKS * C], BF16, align_bytes=64, tag="grouped")
                kept["grouped", h] = grouped
            group_words(nc.scalar.copy, kept["grouped", h], kept["bank", h, pair], pair)

        def quantise(h, pair):
            if pair == 0:
                o_codes = stage.tile([P, BLOCKS * P], U32, align_bytes=64)
                o_scales = stage.tile([P, BLOCKS * P], U8, align_bytes=64)
                kept["codes", h] = o_codes
                kept["scales", h] = o_scales
            quantise_pair(nc, kept["grouped", h], kept["codes", h], kept["scales", h], pair)

        def project(h, pair):
            for a in range(2 * pair, 2 * pair + 2):
                cols = slice(a * P, (a + 1) * P)
                acc = accs.tile([P, C], F32, tag="acc")
                nc.tensor.matmul_mx(
                    out=acc[:],
                    lhsT=kept["codes", h][:, cols].bitcast(FP8X4),
                    lhsT_scale=kept["scales", h][:, cols],
                    rhs=w_codes[:].bitcast(FP8X4),
                    rhs_scale=w_scales[:],
                    start=True,
                    stop=True,
                )
                kept["acc", h, a] = acc

        def image_stats(h):
            if ("stats", h // 2) not in kept:
                t_sum = stats.tile([P, WS], F32)
                dev_sq = stats.tile([P, WS], F32)
                std = stats.tile([P, WS], F32)
                slope = stats.tile([P, WS], F32)
                level = stats.tile([P, WS], F32)
                shifted = stats.tile([P, WS], F32)
                kept["stats", h // 2] = dict(
                    t_sum=t_sum, dev_sq=dev_sq, std=std, slope=slope, level=level, shifted=shifted
                )
            return kept["stats", h // 2]

        def column(h, name, a):
            slot = first_out_slot(h) + a
            return image_stats(h)[name][:, slot : slot + 1]

        def add_bias(h, blocks):
            if ("t", h) not in kept:
                t_all = sums.tile([P, BLOCKS, C], F32)
                kept["t", h] = t_all
            for a in blocks:
                nc.vector.scalar_tensor_tensor(
                    out=kept["t", h][:, a, :],
                    in0=kept["acc", h, a][:],
                    scalar=1.0,
                    in1=bias[:],
                    op0=ALU.mult,
                    op1=ALU.add,
                    accum_out=column(h, "t_sum", a),
                )

        def squared_deviations(h, blocks):
            for a in blocks:
                squares = stage.tile([P, C], BF16)
                nc.scalar.activation(
                    out=squares[:],
                    in_=kept["t", h][:, a, :],
                    func=ACT.Square,
                    bias=column(h, "t_sum", a),
                    scale=-1.0 * C,
                    accum_out=column(h, "dev_sq", a),
                )

        IMAGE = slice(0, WS)

        def standard_deviation(h, cols):
            st = image_stats(h)
            nc.scalar.activation(
                out=st["std"][:, cols],
                in_=st["dev_sq"][:, cols],
                func=ACT.Sqrt,
                scale=1.0 / ((C - 1) * C * C),
            )

        def add_eps(h, cols):
            std = image_stats(h)["std"][:, cols]
            nc.scalar.add(std, std, EPS)

        def slope_step(h, cols, step):
            st = image_stats(h)
            slope = st["slope"][:, cols]
            if step == 0:
                nc.vector.reciprocal(out=slope, in_=st["std"][:, cols])
            if step == 1:
                nc.vector.tensor_mul(out=slope, in0=slope, in1=gain[:, cols])
            if step == 2:
                nc.vector.scalar_tensor_tensor(
                    out=st["level"][:, cols],
                    in0=st["t_sum"][:, cols],
                    scalar=-1.0 / C,
                    in1=slope,
                    op0=ALU.mult,
                    op1=ALU.mult,
                )

        def add_offset(h):
            st = image_stats(h)
            cols = out_slots(h)
            nc.vector.tensor_add(
                out=st["shifted"][:, cols], in0=st["level"][:, cols], in1=offset[:, cols]
            )

        def result_of(h):
            if ("result", h) not in kept:
                result = work.tile([P, BLOCKS, C], F32)
                kept["result", h] = result
            return kept["result", h]

        def scalar_normalise(h, blocks):
            for a in blocks:
                nc.scalar.activation(
                    out=result_of(h)[:, a, :],
                    in_=kept["t", h][:, a, :],
                    func=ACT.Identity,
                    bias=column(h, "shifted", a),
                    scale=column(h, "slope", a),
                )

        def normalise(engine, h, a):
            engine.tensor_scalar(
                out=result_of(h)[:, a, :],
                in0=kept["t", h][:, a, :],
                scalar1=column(h, "slope", a),
                scalar2=column(h, "shifted", a),
                op0=ALU.mult,
                op1=ALU.add,
            )

        def add_x(engine, h, blocks):
            result = kept["result", h]
            engine.tensor_add(
                out=result[:, blocks, :], in0=result[:, blocks, :], in1=kept["x", h][:, blocks, :]
            )

        def copy_x(h, a, pool, tag):
            x_bank = pool.tile([P, C], F32, tag=tag)
            nc.tensor.matmul(
                x_bank[:], lhsT=ident_bf16[:], rhs=kept["x", h][:, a, :], start=True, stop=True
            )
            kept["x_bank", h, a] = x_bank

        def add_copied_x(h, a):
            result = kept["result", h]
            nc.vector.tensor_add(out=result[:, a, :], in0=result[:, a, :], in1=kept["x_bank", h, a][:])

        def add_x_by_psum(h, blocks):
            for a in blocks:
                copy_x(h, a, turn, "turned")
                add_copied_x(h, a)

        def store(h, first, count):
            slot = first_out_slot(h) + first
            nc.sync.dma_start(
                out=out_rows[h // 2, :, slot : slot + count, :],
                in_=kept["result", h][:, first : first + count, :],
            )

        def run(stage_of_half, h, *more):
            if 0 <= h < halves:
                stage_of_half(h, *more)

        turn_bank(0, 0)
        group_bank(0, 0)
        turn_bank(0, 1)
        group_bank(0, 1)
        turn_bank(1, 0)
        for pair in range(PAIRS):
            quantise(0, pair)
            project(0, pair)
        turn_bank(1, 1)
        group_bank(1, 0)
        add_bias(0, (0, 1))
        squared_deviations(0, (0, 1))
        group_bank(1, 1)
        add_bias(0, (2, 3))
        squared_deviations(0, (2, 3))
        turn_bank(2, 0)
        turn_bank(2, 1)
        for pair in range(PAIRS):
            quantise(1, pair)
        for pair in range(PAIRS):
            project(1, pair)

        for i in ROUNDS:
            whole = i - 1 if i % 2 == 0 else -1
            for load, b in later_loads[i - 1 : i]:
                load(b)
            if i > 1:
                squared_deviations(i - 1, range(BLOCKS))
            group_bank(i + 1, 0)
            run(turn_bank, i + 2, 0)
            run(standard_deviation, whole, IMAGE)
            group_bank(i + 1, 1)
            run(turn_bank, i + 2, 1)
            run(add_eps, whole, IMAGE)
            run(scalar_normalise, i - 3, SCALAR_BLOCKS)
            run(copy_x, i - 3, 1, copies, "x_bank")
            add_bias(i, range(BLOCKS))
            run(slope_step, whole, IMAGE, 0)
            quantise(i + 1, 0)
            run(slope_step, whole, IMAGE, 1)
            if i >= 3:
                add_x(nc.vector, i - 3, slice(0, 1))
            run(slope_step, whole, IMAGE, 2)
            quantise(i + 1, 1)
            for pair in range(PAIRS):
                project(i + 1, pair)
            if i == ROUNDS[-1]:
                add_offset(i - 1)
            run(add_offset, i - 2)
            if i >= 3:
                normalise(nc.vector, i - 3, VECTOR_BLOCK)
                add_copied_x(i - 3, 1)
            if i >= 2:
                normalise(nc.gpsimd, i - 2, GPSIMD_BLOCK)
            if i >= 3:
                add_x(nc.gpsimd, i - 3, slice(2, 4))
                store(i - 3, 0, BLOCKS)

        e = halves - 1
        squared_deviations(e - 1, range(BLOCKS))
        scalar_normalise(e - 3, (0, 1, 2))
        add_bias(e, range(BLOCKS))
        for a in range(BLOCKS):
            normalise(nc.gpsimd, e - 2, a)
        squared_deviations(e, range(BLOCKS))
        standard_deviation(e, IMAGE)
        add_eps(e, IMAGE)
        for first in (0, 2):
            add_x_by_psum(e - 3, (first, first + 1))
            store(e - 3, first, 2)
        add_x_by_psum(e - 2, (0, 1))
        store(e - 2, 0, 2)
        slope_step(e, IMAGE, 0)
        add_x_by_psum(e - 2, (2,))
        slope_step(e, IMAGE, 1)
        slope_step(e, IMAGE, 2)
        add_offset(e - 1)
        add_offset(e)
        add_x_by_psum(e - 2, (3,))
        store(e - 2, 2, 2)
        scalar_normalise(e - 1, (0, 1))
        for a in (2, 3):
            normalise(nc.gpsimd, e - 1, a)
        scalar_normalise(e, (0, 1))
        add_x_by_psum(e - 1, (2, 0, 3))
        store(e - 1, 2, 2)
        add_x_by_psum(e - 1, (1,))
        store(e - 1, 0, 2)
        for a in (2, 3):
            normalise(nc.vector, e, a)
        for first in (2, 0):
            for a in (first, first + 1):
                add_x(nc.vector, e, slice(a, a + 1))
            store(e, first, 2)
